import numpy as np
import ml_dtypes


def mxq(x, axis, fmt="e4m3"):
    dtype, down = {"e4m3": (ml_dtypes.float8_e4m3fn, 7), "e5m2": (ml_dtypes.float8_e5m2, 14)}[fmt]
    v = np.moveaxis(np.asarray(x, np.float32).astype(ml_dtypes.bfloat16).astype(np.float64), axis, -1)
    blocks = v.reshape(v.shape[:-1] + (-1, 32))
    amax = np.abs(blocks).max(-1, keepdims=True)
    byte = np.maximum(np.where(amax > 0, np.frexp(amax)[1] - 1 + 127, 0) - down, 1)
    scale = np.exp2(byte - 127.0)
    codes = (blocks / scale).astype(np.float32).astype(dtype).astype(np.float64)
    return np.moveaxis((codes * scale).reshape(v.shape), -1, axis)


WIDE = False


def mx_kscale(k):
    if not WIDE:
        return np.ones(k)
    levels = np.array([10, -10, 5, -5, 0])
    a = np.random.permutation(np.resize(levels, k // 512 * 4)).reshape(k // 512, 4)
    idx = np.arange(k)
    return np.exp2(a[idx // 512, idx % 128 // 32])


BF16 = ml_dtypes.bfloat16


def bf(x):
    return np.asarray(x, np.float32).astype(BF16)


def f64(x):
    return np.asarray(x).astype(np.float64)


E2M1 = np.array([0.0, 0.5, 1.0, 1.5, 2.0, 3.0, 4.0, 6.0, -0.0, -0.5, -1.0, -1.5, -2.0, -3.0, -4.0, -6.0])


def pack_weight(w, fmt):
    k, n = w.shape
    w = f64(bf(w)).reshape(k // 32, 32, n)
    amax = np.abs(w).max(1)
    if fmt == "e4m3":
        byte = np.frexp(amax)[1] - 1 + 127 - 7
    else:
        mant, ex = np.frexp(amax / 6.0)
        byte = np.where(mant > 0.5, ex, ex - 1) + 127
    byte = np.clip(np.where(amax > 0, byte, 1), 1, 254)
    scaled = (w * np.exp2(127.0 - byte)[:, None, :]).reshape(k, n).astype(np.float32)
    by_word = np.ascontiguousarray(scaled.reshape(k // 512, 128, 4, n).transpose(0, 1, 3, 2))
    if fmt == "e4m3":
        words = by_word.astype(ml_dtypes.float8_e4m3fn).view(np.uint8)
    else:
        c = by_word.astype(ml_dtypes.float4_e2m1fn).view(np.uint8) & 0xF
        words = c[..., 0::2] | (c[..., 1::2] << 4)
    return np.ascontiguousarray(words), np.ascontiguousarray(byte.astype(np.uint8).reshape(k // 512, 16, n))


def unpack_weight(words, scales, fmt):
    g, p, n, _ = words.shape
    if fmt == "e4m3":
        vals = np.ascontiguousarray(words).view(ml_dtypes.float8_e4m3fn).astype(np.float64)
    else:
        nib = np.empty((g, p, n, 4), np.uint8)
        nib[..., 0::2] = words & 0xF
        nib[..., 1::2] = words >> 4
        vals = E2M1[nib]
    vals = vals * np.repeat(np.exp2(scales.astype(np.float64) - 127.0), 8, axis=1)[..., None]
    return vals.transpose(0, 1, 3, 2).reshape(g * 512, n)

def pack4(w):
    words, scales = pack_weight(w, "e2m1")
    return words.reshape(words.shape[0], 128, -1), scales


def unpack4(words, scales):
    return unpack_weight(words.reshape(words.shape[0], 128, -1, 2), scales, "e2m1")


B, IN, OUT = 8192, 1024, 128
MU = 0.25


def setup_inputs():
    s = mx_kscale(IN)
    x = np.random.standard_normal((B, IN)) + MU * np.random.standard_normal(IN)
    wa = bf(np.random.standard_normal((OUT, IN)) / MU / s)
    wb = bf(np.random.standard_normal((OUT, IN)) / MU)
    wc = bf(np.random.standard_normal((OUT, IN)) * 12.0 / s)
    wd = bf(np.random.standard_normal((OUT, IN)))
    weight = np.random.standard_normal((OUT, IN)) / np.sqrt(IN) / s
    words, scales = pack4(np.ascontiguousarray(weight.T))
    return {"x": bf(x * s),
            "wa": wa,
            "wb": wb,
            "wc": wc,
            "wd": wd,
            "weight_words": words,
            "weight_scales": scales}


def reference(x, wa, wb, wc, wd, weight_words, weight_scales):
    x_ = f64(x)
    y_ = mxq(x_, 1, "e4m3") @ unpack4(weight_words, weight_scales)
    corr = mxq(y_, 0, "e4m3").T @ mxq(x_, 0, "e4m3")
    dw = (x_.mean(axis=0)[None, :] * f64(wa)
          + y_.mean(axis=0)[:, None] * f64(wb)
          + corr * f64(wc) / B
          + f64(wd))
    return dw

@@ -1,0 +1,267 @@
+from contextlib import ExitStack
+
+import concourse.mybir as mybir
+from concourse.masks import make_identity
+
+F32 = mybir.dt.float32
+BF16 = mybir.dt.bfloat16
+I32 = mybir.dt.int32
+U32 = mybir.dt.uint32
+U8 = mybir.dt.uint8
+FP8X4 = mybir.dt.float8_e4m3fn_x4
+FP4X4 = mybir.dt.float4_e2m1fn_x4
+ALU = mybir.AluOpType
+
+P = 128
+PACK = 4
+K_PASS = P * PACK
+
+BATCH, IN, OUT = 8192, 1024, 128
+CHUNK = K_PASS
+N_CHUNKS = BATCH // CHUNK
+IN_PASSES = IN // K_PASS
+IN_BLOCKS = IN // P
+N_TILE = 512
+N_HALVES = IN // N_TILE
+
+VECTOR_COLS = 640
+SCALAR_PIECE = (IN - VECTOR_COLS) // 2
+
+FLOPS = 2 * 2 * BATCH * IN * OUT
+
+
+def tile_hebbianlinear_pa_t_kernel(tc, x, wa, wb, wc, wd, weight_words, weight_scales, out):
+    nc = tc.nc
+    with ExitStack() as ctx:
+        const = ctx.enter_context(tc.tile_pool(name="const", bufs=1))
+        x_pool = ctx.enter_context(tc.tile_pool(name="x", bufs=4))
+        stage = ctx.enter_context(tc.tile_pool(name="stage", bufs=2))
+        quant = ctx.enter_context(tc.tile_pool(name="quant", bufs=3))
+        psum_xt = ctx.enter_context(tc.psum_pool(name="psum_xt", bufs=4))
+        psum_y = ctx.enter_context(tc.psum_pool(name="psum_y", bufs=1))
+        psum_acc = ctx.enter_context(tc.psum_pool(name="psum_acc", bufs=1))
+        ctx.enter_context(tc.manual_schedule())
+
+        ident = const.tile([P, P], F32)
+        make_identity(nc, ident[:])
+        pick = const.tile([P, IN_BLOCKS, IN_BLOCKS], BF16)
+        nc.vector.memset(pick[:], 0.0)
+        nc.vector.memset(pick[:].rearrange("p a b -> p (a b)")[:, 0 : IN_BLOCKS * IN_BLOCKS : IN_BLOCKS + 1], 1.0)
+        ones = const.tile([P, 2], F32)
+        nc.vector.memset(ones[:], 1.0)
+
+        w_words = const.tile([P, IN_PASSES, 2 * OUT], U8, align_bytes=64)
+        w_scales = const.tile([P, IN_PASSES, OUT], U8, align_bytes=64)
+        nc.vector.memset(w_scales[:].rearrange("p g n -> p (g n)").bitcast(I32), 0)
+
+        x_tiles = {}
+
+        def load_x(c):
+            x_sb = x_pool.tile([P, PACK, IN], BF16)
+            nc.sync.dma_start(
+                out=x_sb[:], in_=x[c * CHUNK : (c + 1) * CHUNK, :].rearrange("(p t) n -> p t n", t=PACK)
+            )
+            x_tiles[c] = x_sb
+
+        load_x(0)
+        nc.sync.dma_start(
+            out=w_words[:].bitcast(I32), in_=weight_words.bitcast(I32).rearrange("g p w -> p g w")
+        )
+        for quadrant in range(4):
+            nc.sync.dma_start(
+                out=w_scales[32 * quadrant : 32 * quadrant + 4].bitcast(I32),
+                in_=weight_scales.bitcast(I32)[:, 4 * quadrant : 4 * quadrant + 4, :].rearrange("g r w -> r g w"),
+            )
+        load_x(1)
+        load_x(2)
+        wa_sb = const.tile([P, IN], BF16)
+        wb_sb = const.tile([P, IN], BF16)
+        wc_sb = const.tile([P, IN], BF16)
+        wd_sb = const.tile([P, IN], BF16)
+
+        corr = [psum_acc.tile([P, N_TILE], F32, name="corr%d" % h) for h in range(N_HALVES)]
+        x_sum = psum_acc.tile([P, N_TILE], F32)
+        y_sum = const.tile([P, PACK, OUT], F32)
+
+        a_group, a_codes, a_scales = {}, {}, {}
+        b_group, b_codes, b_scales = {}, {}, {}
+        y_banks, y_codes, y_scales = {}, {}, {}
+
+        def transpose_slab(c, t):
+            x_sb = x_tiles[c]
+            for j in range(IN_BLOCKS):
+                nc.tensor.matmul(
+                    out=x_sum[:, 0:IN_BLOCKS],
+                    lhsT=x_sb[:, t, j * P : (j + 1) * P],
+                    rhs=pick[:, j, :],
+                    start=(c == 0 and t == 0 and j == 0),
+                    stop=(c == N_CHUNKS - 1 and t == PACK - 1 and j == IN_BLOCKS - 1),
+                )
+            words = x_sb[:, t, :].bitcast(F32)
+            xt = psum_xt.tile([P, IN_PASSES, 2, P], F32, tag="xt")
+            for g in range(IN_PASSES):
+                for u in range(2):
+                    nc.tensor.transpose(xt[:, g, u, :], words[:, 256 * g + u : 256 * (g + 1) : 2], ident[:])
+            if t == 0:
+                a_group[c] = stage.tile([P, PACK, IN_PASSES, P, PACK], BF16, name="a_group", align_bytes=64)
+            nc.scalar.copy(out=a_group[c][:, t].bitcast(F32), in_=xt[:].rearrange("p g u b -> p g b u"))
+
+        def quantise_a(c, half):
+            if half == 0:
+                a_codes[c] = quant.tile([P, PACK * IN_PASSES * P], U32, name="a_codes", align_bytes=64)
+                a_scales[c] = quant.tile([P, PACK * IN_PASSES * P], U8, name="a_scales", align_bytes=64)
+            cols = slice(half * 2 * IN_PASSES * P, (half + 1) * 2 * IN_PASSES * P)
+            nc.vector.quantize_mx(
+                out=a_codes[c][:, cols].bitcast(FP8X4),
+                scales=a_scales[c][:, cols],
+                in_=a_group[c][:, 2 * half : 2 * half + 2].rearrange("p t g b k -> p (t g b k)"),
+            )
+
+        def matmul_1(c):
+            y_ps = psum_y.tile([P, PACK, OUT], F32, tag="y")
+            for t in range(PACK):
+                for g in range(IN_PASSES):
+                    cols = slice((t * IN_PASSES + g) * P, (t * IN_PASSES + g + 1) * P)
+                    nc.tensor.matmul_mx(
+                        out=y_ps[:, t, :],
+                        lhsT=a_codes[c][:, cols].bitcast(FP8X4),
+                        lhsT_scale=a_scales[c][:, cols],
+                        rhs=w_words[:, g, :].bitcast(FP4X4),
+                        rhs_scale=w_scales[:, g, :],
+                        start=(g == 0),
+                        stop=(g == IN_PASSES - 1),
+                    )
+            y_banks[c] = y_ps
+
+        def round_y(c):
+            y_group = stage.tile([P, OUT, PACK], BF16, align_bytes=64)
+            nc.scalar.copy(out=y_group[:], in_=y_banks[c][:].rearrange("p t o -> p o t"))
+            return y_group
+
+        def quantise_y(c, y_group):
+            y_codes[c] = quant.tile([P, OUT], U32, name="y_codes", align_bytes=64)
+            y_scales[c] = quant.tile([P, OUT], U8, name="y_scales", align_bytes=64)
+            nc.vector.quantize_mx(
+                out=y_codes[c][:].bitcast(FP8X4),
+                scales=y_scales[c][:],
+                in_=y_group[:].rearrange("p o t -> p (o t)"),
+            )
+            if c == 0:
+                nc.vector.tensor_copy(out=y_sum[:], in_=y_banks[c][:])
+            else:
+                nc.vector.tensor_tensor(out=y_sum[:], in0=y_banks[c][:], in1=y_sum[:], op=ALU.add)
+
+        def regroup_b(engine_copy, c, first, count):
+            cols = slice(first, first + count)
+            engine_copy(
+                out=b_group[c][:, cols, :].rearrange("p (n i) t -> p n t i", i=4),
+                in_=x_tiles[c][:, :, cols].rearrange("p t (n i) -> p n t i", i=4),
+            )
+
+        def quantise_b(c):
+            b_codes[c] = quant.tile([P, IN], U32, name="b_codes", align_bytes=64)
+            b_scales[c] = quant.tile([P, IN], U8, name="b_scales", align_bytes=64)
+            nc.vector.quantize_mx(
+                out=b_codes[c][:].bitcast(FP8X4),
+                scales=b_scales[c][:],
+                in_=b_group[c][:].rearrange("p n t -> p (n t)"),
+            )
+
+        def matmul_2(c):
+            for h in range(N_HALVES):
+                cols = slice(h * N_TILE, (h + 1) * N_TILE)
+                nc.tensor.matmul_mx(
+                    out=corr[h][:],
+                    lhsT=y_codes[c][:].bitcast(FP8X4),
+                    lhsT_scale=y_scales[c][:],
+                    rhs=b_codes[c][:, cols].bitcast(FP8X4),
+                    rhs_scale=b_scales[c][:, cols],
+                    start=(c == 0),
+                    stop=(c == N_CHUNKS - 1),
+                )
+
+        def step(i):
+            new, mid, old = i, i - 1, i - 2
+            if new + 3 < N_CHUNKS:
+                load_x(new + 3)
+            if mid >= 0:
+                quantise_a(mid, 1)
+            b_group[new] = stage.tile([P, IN, PACK], BF16, name="b_group", align_bytes=64)
+            regroup_b(nc.vector.tensor_copy, new, 0, VECTOR_COLS)
+            transpose_slab(new, 0)
+            transpose_slab(new, 1)
+            regroup_b(nc.scalar.copy, new, VECTOR_COLS, SCALAR_PIECE)
+            quantise_a(new, 0)
+            if mid >= 0:
+                matmul_1(mid)
+                y_group = round_y(mid)
+                quantise_b(mid)
+                quantise_y(mid, y_group)
+            transpose_slab(new, 2)
+            transpose_slab(new, 3)
+            regroup_b(nc.scalar.copy, new, VECTOR_COLS + SCALAR_PIECE, SCALAR_PIECE)
+            if old >= 0:
+                matmul_2(old)
+
+        step(0)
+        nc.sync.dma_start(out=wa_sb[:], in_=wa)
+        nc.sync.dma_start(out=wb_sb[:], in_=wb)
+        nc.sync.dma_start(out=wc_sb[:], in_=wc)
+        nc.sync.dma_start(out=wd_sb[:], in_=wd)
+        for i in range(1, N_CHUNKS):
+            step(i)
+
+        last = N_CHUNKS - 1
+        x_mean = const.tile([P, IN_BLOCKS], F32)
+        nc.vector.tensor_scalar_mul(out=x_mean[:], in0=x_sum[:, 0:IN_BLOCKS], scalar1=1.0 / BATCH)
+        quantise_a(last, 1)
+
+        def spread_x_mean(h):
+            spread = psum_xt.tile([P, N_TILE], F32, tag="xt")
+            for q in range(N_TILE // P):
+                j = h * (N_TILE // P) + q
+                nc.tensor.matmul(
+                    out=spread[:, q * P : (q + 1) * P],
+                    lhsT=x_mean[:, j : j + 1].to_broadcast([P, P]),
+                    rhs=ident[:],
+                    start=True,
+                    stop=True,
+                )
+            return spread
+
+        halves = [slice(h * N_TILE, (h + 1) * N_TILE) for h in range(N_HALVES)]
+        partial = const.tile([P, IN], F32)
+        spread_0 = spread_x_mean(0)
+        matmul_1(last)
+        spread_1 = spread_x_mean(1)
+        y_group = round_y(last)
+        quantise_b(last)
+        nc.vector.tensor_tensor(out=partial[:, halves[0]], in0=spread_0[:], in1=wa_sb[:, halves[0]], op=ALU.mult)
+        nc.vector.tensor_tensor(out=partial[:, halves[1]], in0=spread_1[:], in1=wa_sb[:, halves[1]], op=ALU.mult)
+        nc.gpsimd.tensor_tensor(out=partial[:], in0=partial[:], in1=wd_sb[:], op=ALU.add)
+        quantise_y(last, y_group)
+        matmul_2(last - 1)
+        matmul_2(last)
+
+        y_total = psum_y.tile([P, 2], F32, tag="y")
+        for t in range(PACK):
+            nc.tensor.matmul(
+                out=y_total[:], lhsT=y_sum[:, t, :], rhs=ones[:], start=(t == 0), stop=(t == PACK - 1)
+            )
+        y_mean = const.tile([P, 1], F32)
+        nc.scalar.mul(out=y_mean[:], in_=y_total[:, 0:1], mul=1.0 / BATCH)
+
+        result = const.tile([P, IN], F32)
+        for cols, bank in zip(halves, corr):
+            nc.vector.scalar_tensor_tensor(
+                out=result[:, cols], in0=bank[:], scalar=1.0 / BATCH, in1=wc_sb[:, cols],
+                op0=ALU.mult, op1=ALU.mult,
+            )
+        for cols in halves:
+            nc.vector.tensor_tensor(out=result[:, cols], in0=result[:, cols], in1=partial[:, cols], op=ALU.add)
+        for cols in halves:
+            nc.vector.scalar_tensor_tensor(
+                out=result[:, cols], in0=wb_sb[:, cols], scalar=y_mean[:, 0:1], in1=result[:, cols],
+                op0=ALU.mult, op1=ALU.add,
+            )
+            nc.sync.dma_start(out=out[:, cols], in_=result[:, cols])

@@ -11,6 +11,7 @@ U8 = mybir.dt.uint8
 FP8X4 = mybir.dt.float8_e4m3fn_x4
 FP4X4 = mybir.dt.float4_e2m1fn_x4
 ALU = mybir.AluOpType
+ACT = mybir.ActivationFunctionType
 
 P = 128
 PACK = 4
@@ -24,7 +25,7 @@ IN_BLOCKS = IN // P
 N_TILE = 512
 N_HALVES = IN // N_TILE
 
-VECTOR_COLS = 640
+VECTOR_COLS = 672
 SCALAR_PIECE = (IN - VECTOR_COLS) // 2
 
 FLOPS = 2 * 2 * BATCH * IN * OUT
@@ -37,7 +38,7 @@ def tile_hebbianlinear_pa_t_kernel(tc, x, wa, wb, wc, wd, weight_words, weight_s
         x_pool = ctx.enter_context(tc.tile_pool(name="x", bufs=4))
         stage = ctx.enter_context(tc.tile_pool(name="stage", bufs=2))
         quant = ctx.enter_context(tc.tile_pool(name="quant", bufs=3))
-        psum_xt = ctx.enter_context(tc.psum_pool(name="psum_xt", bufs=4))
+        psum_xt = ctx.enter_context(tc.psum_pool(name="psum_xt", bufs=3))
         psum_y = ctx.enter_context(tc.psum_pool(name="psum_y", bufs=1))
         psum_acc = ctx.enter_context(tc.psum_pool(name="psum_acc", bufs=1))
         ctx.enter_context(tc.manual_schedule())
@@ -47,8 +48,6 @@ def tile_hebbianlinear_pa_t_kernel(tc, x, wa, wb, wc, wd, weight_words, weight_s
         pick = const.tile([P, IN_BLOCKS, IN_BLOCKS], BF16)
         nc.vector.memset(pick[:], 0.0)
         nc.vector.memset(pick[:].rearrange("p a b -> p (a b)")[:, 0 : IN_BLOCKS * IN_BLOCKS : IN_BLOCKS + 1], 1.0)
-        ones = const.tile([P, 2], F32)
-        nc.vector.memset(ones[:], 1.0)
 
         w_words = const.tile([P, IN_PASSES, 2 * OUT], U8, align_bytes=64)
         w_scales = const.tile([P, IN_PASSES, OUT], U8, align_bytes=64)
@@ -56,14 +55,15 @@ def tile_hebbianlinear_pa_t_kernel(tc, x, wa, wb, wc, wd, weight_words, weight_s
 
         x_tiles = {}
 
-        def load_x(c):
+        def load_x(c, pieces):
             x_sb = x_pool.tile([P, PACK, IN], BF16)
-            nc.sync.dma_start(
-                out=x_sb[:], in_=x[c * CHUNK : (c + 1) * CHUNK, :].rearrange("(p t) n -> p t n", t=PACK)
-            )
+            rows = x[c * CHUNK : (c + 1) * CHUNK, :].rearrange("(p t) n -> p t n", t=PACK)
+            step_t = PACK // pieces
+            for t in range(0, PACK, step_t):
+                nc.sync.dma_start(out=x_sb[:, t : t + step_t, :], in_=rows[:, t : t + step_t, :])
             x_tiles[c] = x_sb
 
-        load_x(0)
+        load_x(0, PACK)
         nc.sync.dma_start(
             out=w_words[:].bitcast(I32), in_=weight_words.bitcast(I32).rearrange("g p w -> p g w")
         )
@@ -72,8 +72,8 @@ def tile_hebbianlinear_pa_t_kernel(tc, x, wa, wb, wc, wd, weight_words, weight_s
                 out=w_scales[32 * quadrant : 32 * quadrant + 4].bitcast(I32),
                 in_=weight_scales.bitcast(I32)[:, 4 * quadrant : 4 * quadrant + 4, :].rearrange("g r w -> r g w"),
             )
-        load_x(1)
-        load_x(2)
+        load_x(1, 1)
+        load_x(2, 1)
         wa_sb = const.tile([P, IN], BF16)
         wb_sb = const.tile([P, IN], BF16)
         wc_sb = const.tile([P, IN], BF16)
@@ -81,7 +81,7 @@ def tile_hebbianlinear_pa_t_kernel(tc, x, wa, wb, wc, wd, weight_words, weight_s
 
         corr = [psum_acc.tile([P, N_TILE], F32, name="corr%d" % h) for h in range(N_HALVES)]
         x_sum = psum_acc.tile([P, N_TILE], F32)
-        y_sum = const.tile([P, PACK, OUT], F32)
+        y_cols = psum_acc.tile([P, N_TILE], F32)
 
         a_group, a_codes, a_scales = {}, {}, {}
         b_group, b_codes, b_scales = {}, {}, {}
@@ -103,25 +103,23 @@ def tile_hebbianlinear_pa_t_kernel(tc, x, wa, wb, wc, wd, weight_words, weight_s
                 for u in range(2):
                     nc.tensor.transpose(xt[:, g, u, :], words[:, 256 * g + u : 256 * (g + 1) : 2], ident[:])
             if t == 0:
-                a_group[c] = stage.tile([P, PACK, IN_PASSES, P, PACK], BF16, name="a_group", align_bytes=64)
-            nc.scalar.copy(out=a_group[c][:, t].bitcast(F32), in_=xt[:].rearrange("p g u b -> p g b u"))
+                a_group[c] = stage.tile([P, IN_PASSES, PACK, P, PACK], BF16, name="a_group", align_bytes=64)
+            nc.scalar.copy(out=a_group[c][:, :, t].bitcast(F32), in_=xt[:].rearrange("p g u b -> p g b u"))
 
-        def quantise_a(c, half):
-            if half == 0:
-                a_codes[c] = quant.tile([P, PACK * IN_PASSES * P], U32, name="a_codes", align_bytes=64)
-                a_scales[c] = quant.tile([P, PACK * IN_PASSES * P], U8, name="a_scales", align_bytes=64)
-            cols = slice(half * 2 * IN_PASSES * P, (half + 1) * 2 * IN_PASSES * P)
+        def quantise_a(c):
+            a_codes[c] = quant.tile([P, IN_PASSES * CHUNK], U32, name="a_codes", align_bytes=64)
+            a_scales[c] = quant.tile([P, IN_PASSES * CHUNK], U8, name="a_scales", align_bytes=64)
             nc.vector.quantize_mx(
-                out=a_codes[c][:, cols].bitcast(FP8X4),
-                scales=a_scales[c][:, cols],
-                in_=a_group[c][:, 2 * half : 2 * half + 2].rearrange("p t g b k -> p (t g b k)"),
+                out=a_codes[c][:].bitcast(FP8X4),
+                scales=a_scales[c][:],
+                in_=a_group[c][:].rearrange("p g t b k -> p (g t b k)"),
             )
 
         def matmul_1(c):
             y_ps = psum_y.tile([P, PACK, OUT], F32, tag="y")
             for t in range(PACK):
                 for g in range(IN_PASSES):
-                    cols = slice((t * IN_PASSES + g) * P, (t * IN_PASSES + g + 1) * P)
+                    cols = slice((g * PACK + t) * P, (g * PACK + t + 1) * P)
                     nc.tensor.matmul_mx(
                         out=y_ps[:, t, :],
                         lhsT=a_codes[c][:, cols].bitcast(FP8X4),
@@ -132,6 +130,18 @@ def tile_hebbianlinear_pa_t_kernel(tc, x, wa, wb, wc, wd, weight_words, weight_s
                         stop=(g == IN_PASSES - 1),
                     )
             y_banks[c] = y_ps
+
+        def sum_y(c, g):
+            cols = slice(g * CHUNK, (g + 1) * CHUNK)
+            nc.tensor.matmul_mx(
+                out=y_cols[:],
+                lhsT=w_words[:, g, :].bitcast(FP4X4),
+                lhsT_scale=w_scales[:, g, :],
+                rhs=a_codes[c][:, cols].bitcast(FP8X4),
+                rhs_scale=a_scales[c][:, cols],
+                start=(c == 0 and g == 0),
+                stop=(c == N_CHUNKS - 1 and g == IN_PASSES - 1),
+            )
 
         def round_y(c):
             y_group = stage.tile([P, OUT, PACK], BF16, align_bytes=64)
@@ -146,10 +156,6 @@ def tile_hebbianlinear_pa_t_kernel(tc, x, wa, wb, wc, wd, weight_words, weight_s
                 scales=y_scales[c][:],
                 in_=y_group[:].rearrange("p o t -> p (o t)"),
             )
-            if c == 0:
-                nc.vector.tensor_copy(out=y_sum[:], in_=y_banks[c][:])
-            else:
-                nc.vector.tensor_tensor(out=y_sum[:], in0=y_banks[c][:], in1=y_sum[:], op=ALU.add)
 
         def regroup_b(engine_copy, c, first, count):
             cols = slice(first, first + count)
@@ -183,23 +189,25 @@ def tile_hebbianlinear_pa_t_kernel(tc, x, wa, wb, wc, wd, weight_words, weight_s
         def step(i):
             new, mid, old = i, i - 1, i - 2
             if new + 3 < N_CHUNKS:
-                load_x(new + 3)
+                load_x(new + 3, 1)
             if mid >= 0:
-                quantise_a(mid, 1)
+                quantise_a(mid)
             b_group[new] = stage.tile([P, IN, PACK], BF16, name="b_group", align_bytes=64)
             regroup_b(nc.vector.tensor_copy, new, 0, VECTOR_COLS)
             transpose_slab(new, 0)
             transpose_slab(new, 1)
             regroup_b(nc.scalar.copy, new, VECTOR_COLS, SCALAR_PIECE)
-            quantise_a(new, 0)
             if mid >= 0:
                 matmul_1(mid)
+                sum_y(mid, 0)
                 y_group = round_y(mid)
                 quantise_b(mid)
                 quantise_y(mid, y_group)
             transpose_slab(new, 2)
             transpose_slab(new, 3)
             regroup_b(nc.scalar.copy, new, VECTOR_COLS + SCALAR_PIECE, SCALAR_PIECE)
+            if mid >= 0:
+                sum_y(mid, 1)
             if old >= 0:
                 matmul_2(old)
 
@@ -214,54 +222,50 @@ def tile_hebbianlinear_pa_t_kernel(tc, x, wa, wb, wc, wd, weight_words, weight_s
         last = N_CHUNKS - 1
         x_mean = const.tile([P, IN_BLOCKS], F32)
         nc.vector.tensor_scalar_mul(out=x_mean[:], in0=x_sum[:, 0:IN_BLOCKS], scalar1=1.0 / BATCH)
-        quantise_a(last, 1)
+        quantise_a(last)
 
         def spread_x_mean(h):
-            spread = psum_xt.tile([P, N_TILE], F32, tag="xt")
+            bank = psum_xt.tile([P, N_TILE], F32, tag="xt")
             for q in range(N_TILE // P):
                 j = h * (N_TILE // P) + q
                 nc.tensor.matmul(
-                    out=spread[:, q * P : (q + 1) * P],
+                    out=bank[:, q * P : (q + 1) * P],
                     lhsT=x_mean[:, j : j + 1].to_broadcast([P, P]),
                     rhs=ident[:],
                     start=True,
                     stop=True,
                 )
-            return spread
+            return bank
 
         halves = [slice(h * N_TILE, (h + 1) * N_TILE) for h in range(N_HALVES)]
         partial = const.tile([P, IN], F32)
-        spread_0 = spread_x_mean(0)
+        spread = [spread_x_mean(h) for h in range(N_HALVES)]
         matmul_1(last)
-        spread_1 = spread_x_mean(1)
+        sum_y(last, 0)
+        sum_y(last, 1)
         y_group = round_y(last)
+        y_mean = const.tile([P, 1], F32)
+        y_scaled = const.tile([P, N_TILE], F32)
+        nc.scalar.activation(
+            out=y_scaled[:], in_=y_cols[:], func=ACT.Copy, scale=1.0 / BATCH, accum_out=y_mean[:, 0:1]
+        )
         quantise_b(last)
-        nc.vector.tensor_tensor(out=partial[:, halves[0]], in0=spread_0[:], in1=wa_sb[:, halves[0]], op=ALU.mult)
-        nc.vector.tensor_tensor(out=partial[:, halves[1]], in0=spread_1[:], in1=wa_sb[:, halves[1]], op=ALU.mult)
-        nc.gpsimd.tensor_tensor(out=partial[:], in0=partial[:], in1=wd_sb[:], op=ALU.add)
+        for cols, bank in zip(halves, spread):
+            nc.vector.tensor_tensor(out=partial[:, cols], in0=bank[:], in1=wa_sb[:, cols], op=ALU.mult)
+            nc.gpsimd.tensor_tensor(out=partial[:, cols], in0=partial[:, cols], in1=wd_sb[:, cols], op=ALU.add)
         quantise_y(last, y_group)
         matmul_2(last - 1)
         matmul_2(last)
 
-        y_total = psum_y.tile([P, 2], F32, tag="y")
-        for t in range(PACK):
-            nc.tensor.matmul(
-                out=y_total[:], lhsT=y_sum[:, t, :], rhs=ones[:], start=(t == 0), stop=(t == PACK - 1)
-            )
-        y_mean = const.tile([P, 1], F32)
-        nc.scalar.mul(out=y_mean[:], in_=y_total[:, 0:1], mul=1.0 / BATCH)
-
         result = const.tile([P, IN], F32)
         for cols, bank in zip(halves, corr):
+            nc.vector.scalar_tensor_tensor(
+                out=partial[:, cols], in0=wb_sb[:, cols], scalar=y_mean[:, 0:1], in1=partial[:, cols],
+                op0=ALU.mult, op1=ALU.add,
+            )
             nc.vector.scalar_tensor_tensor(
                 out=result[:, cols], in0=bank[:], scalar=1.0 / BATCH, in1=wc_sb[:, cols],
                 op0=ALU.mult, op1=ALU.mult,
             )
-        for cols in halves:
             nc.vector.tensor_tensor(out=result[:, cols], in0=result[:, cols], in1=partial[:, cols], op=ALU.add)
-        for cols in halves:
-            nc.vector.scalar_tensor_tensor(
-                out=result[:, cols], in0=wb_sb[:, cols], scalar=y_mean[:, 0:1], in1=result[:, cols],
-                op0=ALU.mult, op1=ALU.add,
-            )
             nc.sync.dma_start(out=out[:, cols], in_=result[:, cols])

@@ -11,7 +11,6 @@ U8 = mybir.dt.uint8
 FP8X4 = mybir.dt.float8_e4m3fn_x4
 FP4X4 = mybir.dt.float4_e2m1fn_x4
 ALU = mybir.AluOpType
-ACT = mybir.ActivationFunctionType
 
 P = 128
 PACK = 4
@@ -25,29 +24,37 @@ IN_BLOCKS = IN // P
 N_TILE = 512
 N_HALVES = IN // N_TILE
 
-VECTOR_COLS = 672
+VECTOR_COLS = 592
 SCALAR_PIECE = (IN - VECTOR_COLS) // 2
+SUM_COLS = 16
+LOAD_AHEAD = 5
 
 FLOPS = 2 * 2 * BATCH * IN * OUT
+
+
+def live(c):
+    return 0 <= c < N_CHUNKS
 
 
 def tile_hebbianlinear_pa_t_kernel(tc, x, wa, wb, wc, wd, weight_words, weight_scales, out):
     nc = tc.nc
     with ExitStack() as ctx:
         const = ctx.enter_context(tc.tile_pool(name="const", bufs=1))
-        x_pool = ctx.enter_context(tc.tile_pool(name="x", bufs=4))
-        stage = ctx.enter_context(tc.tile_pool(name="stage", bufs=2))
-        quant = ctx.enter_context(tc.tile_pool(name="quant", bufs=3))
-        psum_xt = ctx.enter_context(tc.psum_pool(name="psum_xt", bufs=3))
+        x_pool = ctx.enter_context(tc.tile_pool(name="x", bufs=LOAD_AHEAD + 1))
+        stage = ctx.enter_context(tc.tile_pool(name="stage", bufs=3))
+        quant = ctx.enter_context(tc.tile_pool(name="quant", bufs=4))
+        psum_xt = ctx.enter_context(tc.psum_pool(name="psum_xt", bufs=4))
         psum_y = ctx.enter_context(tc.psum_pool(name="psum_y", bufs=1))
         psum_acc = ctx.enter_context(tc.psum_pool(name="psum_acc", bufs=1))
         ctx.enter_context(tc.manual_schedule())
 
         ident = const.tile([P, P], F32)
         make_identity(nc, ident[:])
-        pick = const.tile([P, IN_BLOCKS, IN_BLOCKS], BF16)
+        pick = const.tile([P, IN_BLOCKS, SUM_COLS], BF16)
         nc.vector.memset(pick[:], 0.0)
-        nc.vector.memset(pick[:].rearrange("p a b -> p (a b)")[:, 0 : IN_BLOCKS * IN_BLOCKS : IN_BLOCKS + 1], 1.0)
+        nc.vector.memset(pick[:].rearrange("p a b -> p (a b)")[:, 0 : IN_BLOCKS * SUM_COLS : SUM_COLS + 1], 1.0)
+        ones = const.tile([P, 2], F32)
+        nc.vector.memset(ones[:], 1.0)
 
         w_words = const.tile([P, IN_PASSES, 2 * OUT], U8, align_bytes=64)
         w_scales = const.tile([P, IN_PASSES, OUT], U8, align_bytes=64)
@@ -72,39 +79,46 @@ def tile_hebbianlinear_pa_t_kernel(tc, x, wa, wb, wc, wd, weight_words, weight_s
                 out=w_scales[32 * quadrant : 32 * quadrant + 4].bitcast(I32),
                 in_=weight_scales.bitcast(I32)[:, 4 * quadrant : 4 * quadrant + 4, :].rearrange("g r w -> r g w"),
             )
-        load_x(1, 1)
-        load_x(2, 1)
+        for c in range(1, LOAD_AHEAD - 1):
+            load_x(c, 1)
         wa_sb = const.tile([P, IN], BF16)
         wb_sb = const.tile([P, IN], BF16)
         wc_sb = const.tile([P, IN], BF16)
         wd_sb = const.tile([P, IN], BF16)
+        nc.sync.dma_start(out=wa_sb[:], in_=wa)
+        nc.sync.dma_start(out=wb_sb[:], in_=wb)
+        nc.sync.dma_start(out=wc_sb[:], in_=wc)
+        nc.sync.dma_start(out=wd_sb[:], in_=wd)
 
         corr = [psum_acc.tile([P, N_TILE], F32, name="corr%d" % h) for h in range(N_HALVES)]
-        x_sum = psum_acc.tile([P, N_TILE], F32)
-        y_cols = psum_acc.tile([P, N_TILE], F32)
+        x_sum = psum_acc.tile([P, N_TILE], F32, tag="x_sum")
+        y_sum = const.tile([P, PACK, OUT], F32)
 
         a_group, a_codes, a_scales = {}, {}, {}
         b_group, b_codes, b_scales = {}, {}, {}
-        y_banks, y_codes, y_scales = {}, {}, {}
+        y_banks, y_group, y_codes, y_scales = {}, {}, {}, {}
 
-        def transpose_slab(c, t):
-            x_sb = x_tiles[c]
-            for j in range(IN_BLOCKS):
-                nc.tensor.matmul(
-                    out=x_sum[:, 0:IN_BLOCKS],
-                    lhsT=x_sb[:, t, j * P : (j + 1) * P],
-                    rhs=pick[:, j, :],
-                    start=(c == 0 and t == 0 and j == 0),
-                    stop=(c == N_CHUNKS - 1 and t == PACK - 1 and j == IN_BLOCKS - 1),
-                )
-            words = x_sb[:, t, :].bitcast(F32)
-            xt = psum_xt.tile([P, IN_PASSES, 2, P], F32, tag="xt")
-            for g in range(IN_PASSES):
-                for u in range(2):
-                    nc.tensor.transpose(xt[:, g, u, :], words[:, 256 * g + u : 256 * (g + 1) : 2], ident[:])
-            if t == 0:
-                a_group[c] = stage.tile([P, IN_PASSES, PACK, P, PACK], BF16, name="a_group", align_bytes=64)
-            nc.scalar.copy(out=a_group[c][:, :, t].bitcast(F32), in_=xt[:].rearrange("p g u b -> p g b u"))
+        def sum_columns(c, slabs):
+            for t in slabs:
+                for j in range(IN_BLOCKS):
+                    nc.tensor.matmul(
+                        out=x_sum[:, 0:SUM_COLS],
+                        lhsT=x_tiles[c][:, t, j * P : (j + 1) * P],
+                        rhs=pick[:, j, :],
+                        start=(c == 0 and t == 0 and j == 0),
+                        stop=(c == N_CHUNKS - 1 and t == PACK - 1 and j == IN_BLOCKS - 1),
+                    )
+
+        def transpose_slabs(c, slabs):
+            if c not in a_group:
+                a_group[c] = stage.tile([P, PACK, IN_PASSES, P, PACK], BF16, name="a_group", align_bytes=64)
+            for t in slabs:
+                words = x_tiles[c][:, t, :].bitcast(F32)
+                xt = psum_xt.tile([P, IN_PASSES, 2, P], F32, tag="xt")
+                for g in range(IN_PASSES):
+                    for u in range(2):
+                        nc.tensor.transpose(xt[:, g, u, :], words[:, 256 * g + u : 256 * (g + 1) : 2], ident[:])
+                nc.scalar.copy(out=a_group[c][:, t].bitcast(F32), in_=xt[:].rearrange("p g u b -> p g b u"))
 
         def quantise_a(c):
             a_codes[c] = quant.tile([P, IN_PASSES * CHUNK], U32, name="a_codes", align_bytes=64)
@@ -112,16 +126,16 @@ def tile_hebbianlinear_pa_t_kernel(tc, x, wa, wb, wc, wd, weight_words, weight_s
             nc.vector.quantize_mx(
                 out=a_codes[c][:].bitcast(FP8X4),
                 scales=a_scales[c][:],
-                in_=a_group[c][:].rearrange("p g t b k -> p (g t b k)"),
+                in_=a_group[c][:].rearrange("p t g b k -> p (t g b k)"),
             )
 
         def matmul_1(c):
-            y_ps = psum_y.tile([P, PACK, OUT], F32, tag="y")
+            y_banks[c] = psum_y.tile([P, PACK, OUT], F32, name="y_bank", tag="y")
             for t in range(PACK):
                 for g in range(IN_PASSES):
-                    cols = slice((g * PACK + t) * P, (g * PACK + t + 1) * P)
+                    cols = slice((t * IN_PASSES + g) * P, (t * IN_PASSES + g + 1) * P)
                     nc.tensor.matmul_mx(
-                        out=y_ps[:, t, :],
+                        out=y_banks[c][:, t, :],
                         lhsT=a_codes[c][:, cols].bitcast(FP8X4),
                         lhsT_scale=a_scales[c][:, cols],
                         rhs=w_words[:, g, :].bitcast(FP4X4),
@@ -129,35 +143,27 @@ def tile_hebbianlinear_pa_t_kernel(tc, x, wa, wb, wc, wd, weight_words, weight_s
                         start=(g == 0),
                         stop=(g == IN_PASSES - 1),
                     )
-            y_banks[c] = y_ps
-
-        def sum_y(c, g):
-            cols = slice(g * CHUNK, (g + 1) * CHUNK)
-            nc.tensor.matmul_mx(
-                out=y_cols[:],
-                lhsT=w_words[:, g, :].bitcast(FP4X4),
-                lhsT_scale=w_scales[:, g, :],
-                rhs=a_codes[c][:, cols].bitcast(FP8X4),
-                rhs_scale=a_scales[c][:, cols],
-                start=(c == 0 and g == 0),
-                stop=(c == N_CHUNKS - 1 and g == IN_PASSES - 1),
-            )
 
         def round_y(c):
-            y_group = stage.tile([P, OUT, PACK], BF16, align_bytes=64)
-            nc.scalar.copy(out=y_group[:], in_=y_banks[c][:].rearrange("p t o -> p o t"))
-            return y_group
+            y_group[c] = stage.tile([P, OUT, PACK], BF16, name="y_group", align_bytes=64)
+            nc.scalar.copy(out=y_group[c][:], in_=y_banks[c][:].rearrange("p t o -> p o t"))
 
-        def quantise_y(c, y_group):
+        def quantise_y(c):
             y_codes[c] = quant.tile([P, OUT], U32, name="y_codes", align_bytes=64)
             y_scales[c] = quant.tile([P, OUT], U8, name="y_scales", align_bytes=64)
             nc.vector.quantize_mx(
                 out=y_codes[c][:].bitcast(FP8X4),
                 scales=y_scales[c][:],
-                in_=y_group[:].rearrange("p o t -> p (o t)"),
+                in_=y_group[c][:].rearrange("p o t -> p (o t)"),
             )
+            if c == 0:
+                nc.vector.tensor_copy(out=y_sum[:], in_=y_banks[c][:])
+            else:
+                nc.vector.tensor_tensor(out=y_sum[:], in0=y_banks[c][:], in1=y_sum[:], op=ALU.add)
 
         def regroup_b(engine_copy, c, first, count):
+            if c not in b_group:
+                b_group[c] = stage.tile([P, IN, PACK], BF16, name="b_group", align_bytes=64)
             cols = slice(first, first + count)
             engine_copy(
                 out=b_group[c][:, cols, :].rearrange("p (n i) t -> p n t i", i=4),
@@ -187,85 +193,82 @@ def tile_hebbianlinear_pa_t_kernel(tc, x, wa, wb, wc, wd, weight_words, weight_s
                 )
 
         def step(i):
-            new, mid, old = i, i - 1, i - 2
-            if new + 3 < N_CHUNKS:
-                load_x(new + 3, 1)
-            if mid >= 0:
-                quantise_a(mid)
-            b_group[new] = stage.tile([P, IN, PACK], BF16, name="b_group", align_bytes=64)
-            regroup_b(nc.vector.tensor_copy, new, 0, VECTOR_COLS)
-            transpose_slab(new, 0)
-            transpose_slab(new, 1)
-            regroup_b(nc.scalar.copy, new, VECTOR_COLS, SCALAR_PIECE)
-            if mid >= 0:
-                matmul_1(mid)
-                sum_y(mid, 0)
-                y_group = round_y(mid)
-                quantise_b(mid)
-                quantise_y(mid, y_group)
-            transpose_slab(new, 2)
-            transpose_slab(new, 3)
-            regroup_b(nc.scalar.copy, new, VECTOR_COLS + SCALAR_PIECE, SCALAR_PIECE)
-            if mid >= 0:
-                sum_y(mid, 1)
-            if old >= 0:
-                matmul_2(old)
+            if live(i + LOAD_AHEAD):
+                load_x(i + LOAD_AHEAD, 1)
+            if live(i - 1):
+                quantise_a(i - 1)
+            if live(i + 1):
+                regroup_b(nc.vector.tensor_copy, i + 1, 0, VECTOR_COLS)
+            if live(i):
+                transpose_slabs(i, (0, 1))
+            if live(i + 1):
+                sum_columns(i + 1, (0, 1))
+                regroup_b(nc.scalar.copy, i + 1, VECTOR_COLS, SCALAR_PIECE)
+            if live(i - 2):
+                matmul_1(i - 2)
+                round_y(i - 2)
+            if live(i):
+                quantise_b(i)
+            if live(i - 2):
+                quantise_y(i - 2)
+            if live(i):
+                transpose_slabs(i, (2, 3))
+            if live(i + 1):
+                sum_columns(i + 1, (2, 3))
+                regroup_b(nc.scalar.copy, i + 1, VECTOR_COLS + SCALAR_PIECE, SCALAR_PIECE)
+            if live(i - 3):
+                matmul_2(i - 3)
 
-        step(0)
-        nc.sync.dma_start(out=wa_sb[:], in_=wa)
-        nc.sync.dma_start(out=wb_sb[:], in_=wb)
-        nc.sync.dma_start(out=wc_sb[:], in_=wc)
-        nc.sync.dma_start(out=wd_sb[:], in_=wd)
-        for i in range(1, N_CHUNKS):
+        for i in range(-1, N_CHUNKS - 1):
             step(i)
 
-        last = N_CHUNKS - 1
         x_mean = const.tile([P, IN_BLOCKS], F32)
         nc.vector.tensor_scalar_mul(out=x_mean[:], in0=x_sum[:, 0:IN_BLOCKS], scalar1=1.0 / BATCH)
-        quantise_a(last)
+        spread = [
+            psum_acc.tile([P, N_TILE], F32, name="spread0", tag="x_sum"),
+            psum_xt.tile([P, N_TILE], F32, name="spread1", tag="xt"),
+        ]
+        for j in range(IN_BLOCKS):
+            h, q = divmod(j, N_TILE // P)
+            nc.tensor.matmul(
+                out=spread[h][:, q * P : (q + 1) * P],
+                lhsT=x_mean[:, j : j + 1].to_broadcast([P, P]),
+                rhs=ident[:],
+                start=True,
+                stop=True,
+            )
 
-        def spread_x_mean(h):
-            bank = psum_xt.tile([P, N_TILE], F32, tag="xt")
-            for q in range(N_TILE // P):
-                j = h * (N_TILE // P) + q
-                nc.tensor.matmul(
-                    out=bank[:, q * P : (q + 1) * P],
-                    lhsT=x_mean[:, j : j + 1].to_broadcast([P, P]),
-                    rhs=ident[:],
-                    start=True,
-                    stop=True,
-                )
-            return bank
+        step(N_CHUNKS - 1)
+        step(N_CHUNKS)
 
         halves = [slice(h * N_TILE, (h + 1) * N_TILE) for h in range(N_HALVES)]
         partial = const.tile([P, IN], F32)
-        spread = [spread_x_mean(h) for h in range(N_HALVES)]
-        matmul_1(last)
-        sum_y(last, 0)
-        sum_y(last, 1)
-        y_group = round_y(last)
-        y_mean = const.tile([P, 1], F32)
-        y_scaled = const.tile([P, N_TILE], F32)
-        nc.scalar.activation(
-            out=y_scaled[:], in_=y_cols[:], func=ACT.Copy, scale=1.0 / BATCH, accum_out=y_mean[:, 0:1]
-        )
-        quantise_b(last)
         for cols, bank in zip(halves, spread):
             nc.vector.tensor_tensor(out=partial[:, cols], in0=bank[:], in1=wa_sb[:, cols], op=ALU.mult)
             nc.gpsimd.tensor_tensor(out=partial[:, cols], in0=partial[:, cols], in1=wd_sb[:, cols], op=ALU.add)
-        quantise_y(last, y_group)
-        matmul_2(last - 1)
-        matmul_2(last)
+
+        step(N_CHUNKS + 1)
+        step(N_CHUNKS + 2)
+
+        y_total = psum_y.tile([P, 2], F32, tag="y")
+        for t in range(PACK):
+            nc.tensor.matmul(
+                out=y_total[:], lhsT=y_sum[:, t, :], rhs=ones[:], start=(t == 0), stop=(t == PACK - 1)
+            )
+        y_mean = const.tile([P, 1], F32)
+        nc.scalar.mul(out=y_mean[:], in_=y_total[:, 0:1], mul=1.0 / BATCH)
 
         result = const.tile([P, IN], F32)
         for cols, bank in zip(halves, corr):
             nc.vector.scalar_tensor_tensor(
-                out=partial[:, cols], in0=wb_sb[:, cols], scalar=y_mean[:, 0:1], in1=partial[:, cols],
-                op0=ALU.mult, op1=ALU.add,
-            )
-            nc.vector.scalar_tensor_tensor(
                 out=result[:, cols], in0=bank[:], scalar=1.0 / BATCH, in1=wc_sb[:, cols],
                 op0=ALU.mult, op1=ALU.mult,
             )
+        for cols in halves:
             nc.vector.tensor_tensor(out=result[:, cols], in0=result[:, cols], in1=partial[:, cols], op=ALU.add)
+        for cols in halves:
+            nc.vector.scalar_tensor_tensor(
+                out=result[:, cols], in0=wb_sb[:, cols], scalar=y_mean[:, 0:1], in1=result[:, cols],
+                op0=ALU.mult, op1=ALU.add,
+            )
             nc.sync.dma_start(out=out[:, cols], in_=result[:, cols])

@@ -24,7 +24,7 @@ IN_BLOCKS = IN // P
 N_TILE = 512
 N_HALVES = IN // N_TILE
 
-VECTOR_COLS = 592
+VECTOR_COLS = 640
 SCALAR_PIECE = (IN - VECTOR_COLS) // 2
 SUM_COLS = 16
 LOAD_AHEAD = 5

@@ -24,8 +24,8 @@ IN_BLOCKS = IN // P
 N_TILE = 512
 N_HALVES = IN // N_TILE
 
-VECTOR_COLS = 640
-SCALAR_PIECE = (IN - VECTOR_COLS) // 2
+VECTOR_COLS = 608
+SCALAR_PIECE = (IN - VECTOR_COLS) // PACK
 SUM_COLS = 16
 LOAD_AHEAD = 5
 
@@ -71,6 +71,8 @@ def tile_hebbianlinear_pa_t_kernel(tc, x, wa, wb, wc, wd, weight_words, weight_s
             x_tiles[c] = x_sb
 
         load_x(0, PACK)
+        for c in range(1, LOAD_AHEAD - 1):
+            load_x(c, 1)
         nc.sync.dma_start(
             out=w_words[:].bitcast(I32), in_=weight_words.bitcast(I32).rearrange("g p w -> p g w")
         )
@@ -79,16 +81,6 @@ def tile_hebbianlinear_pa_t_kernel(tc, x, wa, wb, wc, wd, weight_words, weight_s
                 out=w_scales[32 * quadrant : 32 * quadrant + 4].bitcast(I32),
                 in_=weight_scales.bitcast(I32)[:, 4 * quadrant : 4 * quadrant + 4, :].rearrange("g r w -> r g w"),
             )
-        for c in range(1, LOAD_AHEAD - 1):
-            load_x(c, 1)
-        wa_sb = const.tile([P, IN], BF16)
-        wb_sb = const.tile([P, IN], BF16)
-        wc_sb = const.tile([P, IN], BF16)
-        wd_sb = const.tile([P, IN], BF16)
-        nc.sync.dma_start(out=wa_sb[:], in_=wa)
-        nc.sync.dma_start(out=wb_sb[:], in_=wb)
-        nc.sync.dma_start(out=wc_sb[:], in_=wc)
-        nc.sync.dma_start(out=wd_sb[:], in_=wd)
 
         corr = [psum_acc.tile([P, N_TILE], F32, name="corr%d" % h) for h in range(N_HALVES)]
         x_sum = psum_acc.tile([P, N_TILE], F32, tag="x_sum")
@@ -199,11 +191,13 @@ def tile_hebbianlinear_pa_t_kernel(tc, x, wa, wb, wc, wd, weight_words, weight_s
                 quantise_a(i - 1)
             if live(i + 1):
                 regroup_b(nc.vector.tensor_copy, i + 1, 0, VECTOR_COLS)
-            if live(i):
-                transpose_slabs(i, (0, 1))
+            for t in (0, 1):
+                if live(i):
+                    transpose_slabs(i, (t,))
+                if live(i + 1):
+                    regroup_b(nc.scalar.copy, i + 1, VECTOR_COLS + t * SCALAR_PIECE, SCALAR_PIECE)
             if live(i + 1):
                 sum_columns(i + 1, (0, 1))
-                regroup_b(nc.scalar.copy, i + 1, VECTOR_COLS, SCALAR_PIECE)
             if live(i - 2):
                 matmul_1(i - 2)
                 round_y(i - 2)
@@ -211,16 +205,27 @@ def tile_hebbianlinear_pa_t_kernel(tc, x, wa, wb, wc, wd, weight_words, weight_s
                 quantise_b(i)
             if live(i - 2):
                 quantise_y(i - 2)
-            if live(i):
-                transpose_slabs(i, (2, 3))
+            for t in (2, 3):
+                if live(i):
+                    transpose_slabs(i, (t,))
+                if live(i + 1):
+                    regroup_b(nc.scalar.copy, i + 1, VECTOR_COLS + t * SCALAR_PIECE, SCALAR_PIECE)
             if live(i + 1):
                 sum_columns(i + 1, (2, 3))
-                regroup_b(nc.scalar.copy, i + 1, VECTOR_COLS + SCALAR_PIECE, SCALAR_PIECE)
             if live(i - 3):
                 matmul_2(i - 3)
 
         for i in range(-1, N_CHUNKS - 1):
             step(i)
+
+        wa_sb = const.tile([P, IN], BF16)
+        wb_sb = const.tile([P, IN], BF16)
+        wc_sb = const.tile([P, IN], BF16)
+        wd_sb = const.tile([P, IN], BF16)
+        nc.sync.dma_start(out=wa_sb[:], in_=wa)
+        nc.sync.dma_start(out=wb_sb[:], in_=wb)
+        nc.sync.dma_start(out=wc_sb[:], in_=wc)
+        nc.sync.dma_start(out=wd_sb[:], in_=wd)
 
         x_mean = const.tile([P, IN_BLOCKS], F32)
         nc.vector.tensor_scalar_mul(out=x_mean[:], in0=x_sum[:, 0:IN_BLOCKS], scalar1=1.0 / BATCH)

@@ -24,7 +24,7 @@ IN_BLOCKS = IN // P
 N_TILE = 512
 N_HALVES = IN // N_TILE
 
-VECTOR_COLS = 608
+VECTOR_COLS = 688
 SCALAR_PIECE = (IN - VECTOR_COLS) // PACK
 SUM_COLS = 16
 LOAD_AHEAD = 5
@@ -43,7 +43,7 @@ def tile_hebbianlinear_pa_t_kernel(tc, x, wa, wb, wc, wd, weight_words, weight_s
         x_pool = ctx.enter_context(tc.tile_pool(name="x", bufs=LOAD_AHEAD + 1))
         stage = ctx.enter_context(tc.tile_pool(name="stage", bufs=3))
         quant = ctx.enter_context(tc.tile_pool(name="quant", bufs=4))
-        psum_xt = ctx.enter_context(tc.psum_pool(name="psum_xt", bufs=4))
+        psum_xt = ctx.enter_context(tc.psum_pool(name="psum_xt", bufs=3))
         psum_y = ctx.enter_context(tc.psum_pool(name="psum_y", bufs=1))
         psum_acc = ctx.enter_context(tc.psum_pool(name="psum_acc", bufs=1))
         ctx.enter_context(tc.manual_schedule())
@@ -53,8 +53,6 @@ def tile_hebbianlinear_pa_t_kernel(tc, x, wa, wb, wc, wd, weight_words, weight_s
         pick = const.tile([P, IN_BLOCKS, SUM_COLS], BF16)
         nc.vector.memset(pick[:], 0.0)
         nc.vector.memset(pick[:].rearrange("p a b -> p (a b)")[:, 0 : IN_BLOCKS * SUM_COLS : SUM_COLS + 1], 1.0)
-        ones = const.tile([P, 2], F32)
-        nc.vector.memset(ones[:], 1.0)
 
         w_words = const.tile([P, IN_PASSES, 2 * OUT], U8, align_bytes=64)
         w_scales = const.tile([P, IN_PASSES, OUT], U8, align_bytes=64)
@@ -84,7 +82,7 @@ def tile_hebbianlinear_pa_t_kernel(tc, x, wa, wb, wc, wd, weight_words, weight_s
 
         corr = [psum_acc.tile([P, N_TILE], F32, name="corr%d" % h) for h in range(N_HALVES)]
         x_sum = psum_acc.tile([P, N_TILE], F32, tag="x_sum")
-        y_sum = const.tile([P, PACK, OUT], F32)
+        y_sum = psum_acc.tile([P, N_TILE], F32, tag="y_sum")
 
         a_group, a_codes, a_scales = {}, {}, {}
         b_group, b_codes, b_scales = {}, {}, {}
@@ -103,14 +101,14 @@ def tile_hebbianlinear_pa_t_kernel(tc, x, wa, wb, wc, wd, weight_words, weight_s
 
         def transpose_slabs(c, slabs):
             if c not in a_group:
-                a_group[c] = stage.tile([P, PACK, IN_PASSES, P, PACK], BF16, name="a_group", align_bytes=64)
+                a_group[c] = stage.tile([P, IN_PASSES, PACK, P, PACK], BF16, name="a_group", align_bytes=64)
             for t in slabs:
                 words = x_tiles[c][:, t, :].bitcast(F32)
                 xt = psum_xt.tile([P, IN_PASSES, 2, P], F32, tag="xt")
                 for g in range(IN_PASSES):
                     for u in range(2):
                         nc.tensor.transpose(xt[:, g, u, :], words[:, 256 * g + u : 256 * (g + 1) : 2], ident[:])
-                nc.scalar.copy(out=a_group[c][:, t].bitcast(F32), in_=xt[:].rearrange("p g u b -> p g b u"))
+                nc.scalar.copy(out=a_group[c][:, :, t].bitcast(F32), in_=xt[:].rearrange("p g u b -> p g b u"))
 
         def quantise_a(c):
             a_codes[c] = quant.tile([P, IN_PASSES * CHUNK], U32, name="a_codes", align_bytes=64)
@@ -118,14 +116,14 @@ def tile_hebbianlinear_pa_t_kernel(tc, x, wa, wb, wc, wd, weight_words, weight_s
             nc.vector.quantize_mx(
                 out=a_codes[c][:].bitcast(FP8X4),
                 scales=a_scales[c][:],
-                in_=a_group[c][:].rearrange("p t g b k -> p (t g b k)"),
+                in_=a_group[c][:].rearrange("p g t b k -> p (g t b k)"),
             )
 
         def matmul_1(c):
             y_banks[c] = psum_y.tile([P, PACK, OUT], F32, name="y_bank", tag="y")
             for t in range(PACK):
                 for g in range(IN_PASSES):
-                    cols = slice((t * IN_PASSES + g) * P, (t * IN_PASSES + g + 1) * P)
+                    cols = slice((g * PACK + t) * P, (g * PACK + t + 1) * P)
                     nc.tensor.matmul_mx(
                         out=y_banks[c][:, t, :],
                         lhsT=a_codes[c][:, cols].bitcast(FP8X4),
@@ -135,6 +133,19 @@ def tile_hebbianlinear_pa_t_kernel(tc, x, wa, wb, wc, wd, weight_words, weight_s
                         start=(g == 0),
                         stop=(g == IN_PASSES - 1),
                     )
+
+        def sum_y(c):
+            for g in range(IN_PASSES):
+                cols = slice(g * CHUNK, (g + 1) * CHUNK)
+                nc.tensor.matmul_mx(
+                    out=y_sum[:],
+                    lhsT=w_words[:, g, :].bitcast(FP4X4),
+                    lhsT_scale=w_scales[:, g, :],
+                    rhs=a_codes[c][:, cols].bitcast(FP8X4),
+                    rhs_scale=a_scales[c][:, cols],
+                    start=(c == 0 and g == 0),
+                    stop=(c == N_CHUNKS - 1 and g == IN_PASSES - 1),
+                )
 
         def round_y(c):
             y_group[c] = stage.tile([P, OUT, PACK], BF16, name="y_group", align_bytes=64)
@@ -148,10 +159,6 @@ def tile_hebbianlinear_pa_t_kernel(tc, x, wa, wb, wc, wd, weight_words, weight_s
                 scales=y_scales[c][:],
                 in_=y_group[c][:].rearrange("p o t -> p (o t)"),
             )
-            if c == 0:
-                nc.vector.tensor_copy(out=y_sum[:], in_=y_banks[c][:])
-            else:
-                nc.vector.tensor_tensor(out=y_sum[:], in0=y_banks[c][:], in1=y_sum[:], op=ALU.add)
 
         def regroup_b(engine_copy, c, first, count):
             if c not in b_group:
@@ -200,6 +207,7 @@ def tile_hebbianlinear_pa_t_kernel(tc, x, wa, wb, wc, wd, weight_words, weight_s
                 sum_columns(i + 1, (0, 1))
             if live(i - 2):
                 matmul_1(i - 2)
+                sum_y(i - 2)
                 round_y(i - 2)
             if live(i):
                 quantise_b(i)
@@ -253,15 +261,15 @@ def tile_hebbianlinear_pa_t_kernel(tc, x, wa, wb, wc, wd, weight_words, weight_s
             nc.gpsimd.tensor_tensor(out=partial[:, cols], in0=partial[:, cols], in1=wd_sb[:, cols], op=ALU.add)
 
         step(N_CHUNKS + 1)
-        step(N_CHUNKS + 2)
 
-        y_total = psum_y.tile([P, 2], F32, tag="y")
-        for t in range(PACK):
-            nc.tensor.matmul(
-                out=y_total[:], lhsT=y_sum[:, t, :], rhs=ones[:], start=(t == 0), stop=(t == PACK - 1)
-            )
         y_mean = const.tile([P, 1], F32)
-        nc.scalar.mul(out=y_mean[:], in_=y_total[:, 0:1], mul=1.0 / BATCH)
+        y_scaled = const.tile([P, N_TILE], F32)
+        nc.scalar.activation(
+            out=y_scaled[:], in_=y_sum[:], func=mybir.ActivationFunctionType.Copy, scale=1.0 / BATCH,
+            accum_out=y_mean[:],
+        )
+
+        step(N_CHUNKS + 2)
 
         result = const.tile([P, IN], F32)
         for cols, bank in zip(halves, corr):

@@ -25,7 +25,8 @@ N_TILE = 512
 N_HALVES = IN // N_TILE
 
 VECTOR_COLS = 688
-SCALAR_PIECE = (IN - VECTOR_COLS) // PACK
+FIRST_VECTOR_COLS = 960
+LAST_VECTOR_COLS = 496
 SUM_COLS = 16
 LOAD_AHEAD = 5
 
@@ -34,6 +35,14 @@ FLOPS = 2 * 2 * BATCH * IN * OUT
 
 def live(c):
     return 0 <= c < N_CHUNKS
+
+
+def vector_cols(c):
+    if c == 0:
+        return FIRST_VECTOR_COLS
+    if c == N_CHUNKS - 1:
+        return LAST_VECTOR_COLS
+    return VECTOR_COLS
 
 
 def tile_hebbianlinear_pa_t_kernel(tc, x, wa, wb, wc, wd, weight_words, weight_scales, out):
@@ -69,7 +78,7 @@ def tile_hebbianlinear_pa_t_kernel(tc, x, wa, wb, wc, wd, weight_words, weight_s
             x_tiles[c] = x_sb
 
         load_x(0, PACK)
-        for c in range(1, LOAD_AHEAD - 1):
+        for c in range(1, 3):
             load_x(c, 1)
         nc.sync.dma_start(
             out=w_words[:].bitcast(I32), in_=weight_words.bitcast(I32).rearrange("g p w -> p g w")
@@ -79,6 +88,9 @@ def tile_hebbianlinear_pa_t_kernel(tc, x, wa, wb, wc, wd, weight_words, weight_s
                 out=w_scales[32 * quadrant : 32 * quadrant + 4].bitcast(I32),
                 in_=weight_scales.bitcast(I32)[:, 4 * quadrant : 4 * quadrant + 4, :].rearrange("g r w -> r g w"),
             )
+
+        for c in range(3, LOAD_AHEAD):
+            load_x(c, 1)
 
         corr = [psum_acc.tile([P, N_TILE], F32, name="corr%d" % h) for h in range(N_HALVES)]
         x_sum = psum_acc.tile([P, N_TILE], F32, tag="x_sum")
@@ -191,39 +203,71 @@ def tile_hebbianlinear_pa_t_kernel(tc, x, wa, wb, wc, wd, weight_words, weight_s
                     stop=(c == N_CHUNKS - 1),
                 )
 
+        def regroup_vector(c):
+            regroup_b(nc.vector.tensor_copy, c, 0, vector_cols(c))
+
+        def regroup_scalar(c, piece):
+            count = (IN - vector_cols(c)) // PACK
+            regroup_b(nc.scalar.copy, c, vector_cols(c) + piece * count, count)
+
+        LAST = N_CHUNKS - 1
+
         def step(i):
             if live(i + LOAD_AHEAD):
                 load_x(i + LOAD_AHEAD, 1)
             if live(i - 1):
                 quantise_a(i - 1)
-            if live(i + 1):
-                regroup_b(nc.vector.tensor_copy, i + 1, 0, VECTOR_COLS)
+            if i < LAST:
+                regroup_vector(i)
+            else:
+                nc.vector.tensor_scalar_mul(out=x_mean[:], in0=x_sum[:, 0:IN_BLOCKS], scalar1=1.0 / BATCH)
             for t in (0, 1):
-                if live(i):
-                    transpose_slabs(i, (t,))
-                if live(i + 1):
-                    regroup_b(nc.scalar.copy, i + 1, VECTOR_COLS + t * SCALAR_PIECE, SCALAR_PIECE)
-            if live(i + 1):
+                transpose_slabs(i, (t,))
+                if i < LAST:
+                    regroup_scalar(i, t)
+            if i == 0:
+                sum_columns(0, (0, 1))
+            elif live(i + 1):
                 sum_columns(i + 1, (0, 1))
+            else:
+                spread_x_mean(0)
             if live(i - 2):
                 matmul_1(i - 2)
                 sum_y(i - 2)
                 round_y(i - 2)
-            if live(i):
-                quantise_b(i)
+            if live(i - 1):
+                quantise_b(i - 1)
             if live(i - 2):
                 quantise_y(i - 2)
             for t in (2, 3):
-                if live(i):
-                    transpose_slabs(i, (t,))
-                if live(i + 1):
-                    regroup_b(nc.scalar.copy, i + 1, VECTOR_COLS + t * SCALAR_PIECE, SCALAR_PIECE)
-            if live(i + 1):
+                transpose_slabs(i, (t,))
+                if i < LAST:
+                    regroup_scalar(i, t)
+            if i == 0:
+                sum_columns(0, (2, 3))
+                sum_columns(1, (0, 1, 2, 3))
+            elif live(i + 1):
                 sum_columns(i + 1, (2, 3))
+            else:
+                spread_x_mean(1)
             if live(i - 3):
                 matmul_2(i - 3)
 
-        for i in range(-1, N_CHUNKS - 1):
+        x_mean = const.tile([P, IN_BLOCKS], F32)
+        spread = {}
+
+        def spread_x_mean(h):
+            if h == 0:
+                spread[h] = psum_acc.tile([P, N_TILE], F32, name="spread0", tag="x_sum")
+            else:
+                spread[h] = psum_xt.tile([P, N_TILE], F32, name="spread1", tag="xt")
+            for q in range(N_TILE // P):
+                j = h * (N_TILE // P) + q
+                nc.tensor.transpose(
+                    spread[h][:, q * P : (q + 1) * P], x_mean[:, j : j + 1].to_broadcast([P, P]), ident[:]
+                )
+
+        for i in range(0, N_CHUNKS - LOAD_AHEAD):
             step(i)
 
         wa_sb = const.tile([P, IN], BF16)
@@ -235,53 +279,53 @@ def tile_hebbianlinear_pa_t_kernel(tc, x, wa, wb, wc, wd, weight_words, weight_s
         nc.sync.dma_start(out=wc_sb[:], in_=wc)
         nc.sync.dma_start(out=wd_sb[:], in_=wd)
 
-        x_mean = const.tile([P, IN_BLOCKS], F32)
-        nc.vector.tensor_scalar_mul(out=x_mean[:], in0=x_sum[:, 0:IN_BLOCKS], scalar1=1.0 / BATCH)
-        spread = [
-            psum_acc.tile([P, N_TILE], F32, name="spread0", tag="x_sum"),
-            psum_xt.tile([P, N_TILE], F32, name="spread1", tag="xt"),
-        ]
-        for j in range(IN_BLOCKS):
-            h, q = divmod(j, N_TILE // P)
-            nc.tensor.matmul(
-                out=spread[h][:, q * P : (q + 1) * P],
-                lhsT=x_mean[:, j : j + 1].to_broadcast([P, P]),
-                rhs=ident[:],
-                start=True,
-                stop=True,
-            )
+        for i in range(N_CHUNKS - LOAD_AHEAD, LAST):
+            step(i)
 
-        step(N_CHUNKS - 1)
-        step(N_CHUNKS)
+        step(LAST)
 
         halves = [slice(h * N_TILE, (h + 1) * N_TILE) for h in range(N_HALVES)]
-        partial = const.tile([P, IN], F32)
-        for cols, bank in zip(halves, spread):
-            nc.vector.tensor_tensor(out=partial[:, cols], in0=bank[:], in1=wa_sb[:, cols], op=ALU.mult)
-            nc.gpsimd.tensor_tensor(out=partial[:, cols], in0=partial[:, cols], in1=wd_sb[:, cols], op=ALU.add)
-
-        step(N_CHUNKS + 1)
-
+        rest = const.tile([P, IN], F32)
+        result = const.tile([P, IN], F32)
         y_mean = const.tile([P, 1], F32)
         y_scaled = const.tile([P, N_TILE], F32)
+
+        quantise_a(LAST)
+        regroup_vector(LAST)
+        regroup_scalar(LAST, 0)
+        regroup_scalar(LAST, 1)
+        matmul_1(LAST - 1)
+        sum_y(LAST - 1)
+        round_y(LAST - 1)
+        regroup_scalar(LAST, 2)
+        regroup_scalar(LAST, 3)
+        matmul_1(LAST)
+        sum_y(LAST)
+        round_y(LAST)
+        matmul_2(LAST - 2)
+        quantise_y(LAST - 1)
+        matmul_2(LAST - 1)
         nc.scalar.activation(
             out=y_scaled[:], in_=y_sum[:], func=mybir.ActivationFunctionType.Copy, scale=1.0 / BATCH,
             accum_out=y_mean[:],
         )
+        for h, cols in enumerate(halves):
+            nc.vector.tensor_tensor(out=rest[:, cols], in0=spread[h][:], in1=wa_sb[:, cols], op=ALU.mult)
+        quantise_b(LAST)
+        quantise_y(LAST)
+        matmul_2(LAST)
+        for cols in halves:
+            nc.vector.tensor_tensor(out=rest[:, cols], in0=rest[:, cols], in1=wd_sb[:, cols], op=ALU.add)
+        for cols in halves:
+            nc.vector.scalar_tensor_tensor(
+                out=rest[:, cols], in0=wb_sb[:, cols], scalar=y_mean[:, 0:1], in1=rest[:, cols],
+                op0=ALU.mult, op1=ALU.add,
+            )
 
-        step(N_CHUNKS + 2)
-
-        result = const.tile([P, IN], F32)
         for cols, bank in zip(halves, corr):
             nc.vector.scalar_tensor_tensor(
                 out=result[:, cols], in0=bank[:], scalar=1.0 / BATCH, in1=wc_sb[:, cols],
                 op0=ALU.mult, op1=ALU.mult,
             )
-        for cols in halves:
-            nc.vector.tensor_tensor(out=result[:, cols], in0=result[:, cols], in1=partial[:, cols], op=ALU.add)
-        for cols in halves:
-            nc.vector.scalar_tensor_tensor(
-                out=result[:, cols], in0=wb_sb[:, cols], scalar=y_mean[:, 0:1], in1=result[:, cols],
-                op0=ALU.mult, op1=ALU.add,
-            )
+            nc.vector.tensor_tensor(out=result[:, cols], in0=result[:, cols], in1=rest[:, cols], op=ALU.add)
             nc.sync.dma_start(out=out[:, cols], in_=result[:, cols])

@@ -26,7 +26,6 @@ N_HALVES = IN // N_TILE
 
 VECTOR_COLS = 688
 FIRST_VECTOR_COLS = 960
-LAST_VECTOR_COLS = 496
 SUM_COLS = 16
 LOAD_AHEAD = 5
 
@@ -40,8 +39,6 @@ def live(c):
 def vector_cols(c):
     if c == 0:
         return FIRST_VECTOR_COLS
-    if c == N_CHUNKS - 1:
-        return LAST_VECTOR_COLS
     return VECTOR_COLS
 
 
@@ -59,6 +56,8 @@ def tile_hebbianlinear_pa_t_kernel(tc, x, wa, wb, wc, wd, weight_words, weight_s
 
         ident = const.tile([P, P], F32)
         make_identity(nc, ident[:])
+        ident_bf = const.tile([P, P], BF16)
+        make_identity(nc, ident_bf[:])
         pick = const.tile([P, IN_BLOCKS, SUM_COLS], BF16)
         nc.vector.memset(pick[:], 0.0)
         nc.vector.memset(pick[:].rearrange("p a b -> p (a b)")[:, 0 : IN_BLOCKS * SUM_COLS : SUM_COLS + 1], 1.0)
@@ -217,20 +216,18 @@ def tile_hebbianlinear_pa_t_kernel(tc, x, wa, wb, wc, wd, weight_words, weight_s
                 load_x(i + LOAD_AHEAD, 1)
             if live(i - 1):
                 quantise_a(i - 1)
-            if i < LAST:
-                regroup_vector(i)
-            else:
+            if i == LAST:
                 nc.vector.tensor_scalar_mul(out=x_mean[:], in0=x_sum[:, 0:IN_BLOCKS], scalar1=1.0 / BATCH)
+            regroup_vector(i)
             for t in (0, 1):
                 transpose_slabs(i, (t,))
-                if i < LAST:
-                    regroup_scalar(i, t)
+                regroup_scalar(i, t)
             if i == 0:
                 sum_columns(0, (0, 1))
             elif live(i + 1):
                 sum_columns(i + 1, (0, 1))
             else:
-                spread_x_mean(0)
+                transpose_wa()
             if live(i - 2):
                 matmul_1(i - 2)
                 sum_y(i - 2)
@@ -241,84 +238,89 @@ def tile_hebbianlinear_pa_t_kernel(tc, x, wa, wb, wc, wd, weight_words, weight_s
                 quantise_y(i - 2)
             for t in (2, 3):
                 transpose_slabs(i, (t,))
-                if i < LAST:
-                    regroup_scalar(i, t)
+                regroup_scalar(i, t)
             if i == 0:
                 sum_columns(0, (2, 3))
                 sum_columns(1, (0, 1, 2, 3))
             elif live(i + 1):
                 sum_columns(i + 1, (2, 3))
             else:
-                spread_x_mean(1)
+                start_rest()
             if live(i - 3):
                 matmul_2(i - 3)
 
+        halves = [slice(h * N_TILE, (h + 1) * N_TILE) for h in range(N_HALVES)]
         x_mean = const.tile([P, IN_BLOCKS], F32)
-        spread = {}
+        wa_sb = const.tile([P, IN], BF16)
+        wb_sb = const.tile([P, IN], BF16)
+        wc_sb = const.tile([P, IN], BF16)
+        wd_sb = const.tile([P, IN], BF16)
+        wa_t, rest_ps = {}, {}
+        xa_t = const.tile([P, IN_BLOCKS, P], F32)
 
-        def spread_x_mean(h):
-            if h == 0:
-                spread[h] = psum_acc.tile([P, N_TILE], F32, name="spread0", tag="x_sum")
-            else:
-                spread[h] = psum_xt.tile([P, N_TILE], F32, name="spread1", tag="xt")
-            for q in range(N_TILE // P):
-                j = h * (N_TILE // P) + q
-                nc.tensor.transpose(
-                    spread[h][:, q * P : (q + 1) * P], x_mean[:, j : j + 1].to_broadcast([P, P]), ident[:]
+        def transpose_wa():
+            wa_t[0] = psum_acc.tile([P, IN_BLOCKS, P], BF16, name="wa_t", tag="x_sum")
+            for j in range(IN_BLOCKS):
+                nc.tensor.transpose(wa_t[0][:, j, :], wa_sb[:, j * P : (j + 1) * P], ident_bf[:])
+
+        def start_rest():
+            for h, cols in enumerate(halves):
+                rest_ps[h] = psum_xt.tile([P, N_TILE], F32, name="rest_ps%d" % h, tag="xt")
+                nc.tensor.matmul(out=rest_ps[h][:], lhsT=ident_bf[:], rhs=wd_sb[:, cols], start=True, stop=False)
+
+        def scale_wa(blocks):
+            for j in blocks:
+                nc.scalar.activation(
+                    out=xa_t[:, j, :], in_=wa_t[0][:, j, :], func=mybir.ActivationFunctionType.Copy,
+                    scale=x_mean[:, j : j + 1],
+                )
+
+        def finish_rest():
+            for j in range(IN_BLOCKS):
+                h, q = divmod(j, N_TILE // P)
+                nc.tensor.matmul(
+                    out=rest_ps[h][:, q * P : (q + 1) * P], lhsT=xa_t[:, j, :], rhs=ident[:], is_transpose=True,
+                    start=False, stop=(q == N_TILE // P - 1),
                 )
 
         for i in range(0, N_CHUNKS - LOAD_AHEAD):
             step(i)
 
-        wa_sb = const.tile([P, IN], BF16)
-        wb_sb = const.tile([P, IN], BF16)
-        wc_sb = const.tile([P, IN], BF16)
-        wd_sb = const.tile([P, IN], BF16)
         nc.sync.dma_start(out=wa_sb[:], in_=wa)
+        nc.sync.dma_start(out=wd_sb[:], in_=wd)
         nc.sync.dma_start(out=wb_sb[:], in_=wb)
         nc.sync.dma_start(out=wc_sb[:], in_=wc)
-        nc.sync.dma_start(out=wd_sb[:], in_=wd)
 
-        for i in range(N_CHUNKS - LOAD_AHEAD, LAST):
+        for i in range(N_CHUNKS - LOAD_AHEAD, N_CHUNKS):
             step(i)
 
-        step(LAST)
-
-        halves = [slice(h * N_TILE, (h + 1) * N_TILE) for h in range(N_HALVES)]
         rest = const.tile([P, IN], F32)
         result = const.tile([P, IN], F32)
         y_mean = const.tile([P, 1], F32)
         y_scaled = const.tile([P, N_TILE], F32)
 
         quantise_a(LAST)
-        regroup_vector(LAST)
-        regroup_scalar(LAST, 0)
-        regroup_scalar(LAST, 1)
         matmul_1(LAST - 1)
         sum_y(LAST - 1)
         round_y(LAST - 1)
-        regroup_scalar(LAST, 2)
-        regroup_scalar(LAST, 3)
-        matmul_1(LAST)
-        sum_y(LAST)
-        round_y(LAST)
+        scale_wa(range(IN_BLOCKS))
         matmul_2(LAST - 2)
         quantise_y(LAST - 1)
-        matmul_2(LAST - 1)
+        quantise_b(LAST)
+        matmul_1(LAST)
+        round_y(LAST)
+        sum_y(LAST)
+        finish_rest()
         nc.scalar.activation(
             out=y_scaled[:], in_=y_sum[:], func=mybir.ActivationFunctionType.Copy, scale=1.0 / BATCH,
             accum_out=y_mean[:],
         )
-        for h, cols in enumerate(halves):
-            nc.vector.tensor_tensor(out=rest[:, cols], in0=spread[h][:], in1=wa_sb[:, cols], op=ALU.mult)
-        quantise_b(LAST)
+        matmul_2(LAST - 1)
         quantise_y(LAST)
         matmul_2(LAST)
-        for cols in halves:
-            nc.vector.tensor_tensor(out=rest[:, cols], in0=rest[:, cols], in1=wd_sb[:, cols], op=ALU.add)
-        for cols in halves:
+        for h, cols in enumerate(halves):
             nc.vector.scalar_tensor_tensor(
-                out=rest[:, cols], in0=wb_sb[:, cols], scalar=y_mean[:, 0:1], in1=rest[:, cols],
+                out=rest[:, cols], in0=wb_sb[:, cols], scalar=y_mean[:, 0:1], in1=rest_ps[h][:],
                 op0=ALU.mult, op1=ALU.add,
             )
 

@@ -54,6 +54,16 @@ def tile_hebbianlinear_pa_t_kernel(tc, x, wa, wb, wc, wd, weight_words, weight_s
         psum_acc = ctx.enter_context(tc.psum_pool(name="psum_acc", bufs=1))
         ctx.enter_context(tc.manual_schedule())
 
+        zeros = const.tile([P, N_TILE], BF16)
+        nc.vector.memset(zeros[:], 0.0)
+
+        def keep_warm(count):
+            warm = psum_y.tile([P, N_TILE], F32, name="warm", tag="y")
+            for repeat in range(count):
+                nc.tensor.matmul(out=warm[:], lhsT=zeros[:, 0:P], rhs=zeros[:], start=True, stop=True)
+
+        keep_warm(2)
+
         ident = const.tile([P, P], F32)
         make_identity(nc, ident[:])
         ident_bf = const.tile([P, P], BF16)
@@ -232,6 +242,8 @@ def tile_hebbianlinear_pa_t_kernel(tc, x, wa, wb, wc, wd, weight_words, weight_s
                 matmul_1(i - 2)
                 sum_y(i - 2)
                 round_y(i - 2)
+            else:
+                keep_warm(1)
             if live(i - 1):
                 quantise_b(i - 1)
             if live(i - 2):
@@ -248,6 +260,8 @@ def tile_hebbianlinear_pa_t_kernel(tc, x, wa, wb, wc, wd, weight_words, weight_s
                 start_rest()
             if live(i - 3):
                 matmul_2(i - 3)
+            else:
+                keep_warm(1)
 
         halves = [slice(h * N_TILE, (h + 1) * N_TILE) for h in range(N_HALVES)]
         x_mean = const.tile([P, IN_BLOCKS], F32)

@@ -27,7 +27,7 @@ N_HALVES = IN // N_TILE
 VECTOR_COLS = 688
 FIRST_VECTOR_COLS = 960
 SUM_COLS = 16
-LOAD_AHEAD = 5
+LOAD_AHEAD = 6
 
 FLOPS = 2 * 2 * BATCH * IN * OUT
 
@@ -47,8 +47,8 @@ def tile_hebbianlinear_pa_t_kernel(tc, x, wa, wb, wc, wd, weight_words, weight_s
     with ExitStack() as ctx:
         const = ctx.enter_context(tc.tile_pool(name="const", bufs=1))
         x_pool = ctx.enter_context(tc.tile_pool(name="x", bufs=LOAD_AHEAD + 1))
-        stage = ctx.enter_context(tc.tile_pool(name="stage", bufs=3))
-        quant = ctx.enter_context(tc.tile_pool(name="quant", bufs=4))
+        stage = ctx.enter_context(tc.tile_pool(name="stage", bufs=4))
+        quant = ctx.enter_context(tc.tile_pool(name="quant", bufs=5))
         psum_xt = ctx.enter_context(tc.psum_pool(name="psum_xt", bufs=3))
         psum_y = ctx.enter_context(tc.psum_pool(name="psum_y", bufs=1))
         psum_acc = ctx.enter_context(tc.psum_pool(name="psum_acc", bufs=1))
@@ -155,8 +155,8 @@ def tile_hebbianlinear_pa_t_kernel(tc, x, wa, wb, wc, wd, weight_words, weight_s
                         stop=(g == IN_PASSES - 1),
                     )
 
-        def sum_y(c):
-            for g in range(IN_PASSES):
+        def sum_y(c, passes=(0, 1)):
+            for g in passes:
                 cols = slice(g * CHUNK, (g + 1) * CHUNK)
                 nc.tensor.matmul_mx(
                     out=y_sum[:],
@@ -216,7 +216,7 @@ def tile_hebbianlinear_pa_t_kernel(tc, x, wa, wb, wc, wd, weight_words, weight_s
             regroup_b(nc.vector.tensor_copy, c, 0, vector_cols(c))
 
         def regroup_scalar(c, piece):
-            count = (IN - vector_cols(c)) // PACK
+            count = (IN - vector_cols(c)) // 2
             regroup_b(nc.scalar.copy, c, vector_cols(c) + piece * count, count)
 
         LAST = N_CHUNKS - 1
@@ -229,9 +229,8 @@ def tile_hebbianlinear_pa_t_kernel(tc, x, wa, wb, wc, wd, weight_words, weight_s
             if i == LAST:
                 nc.vector.tensor_scalar_mul(out=x_mean[:], in0=x_sum[:, 0:IN_BLOCKS], scalar1=1.0 / BATCH)
             regroup_vector(i)
-            for t in (0, 1):
-                transpose_slabs(i, (t,))
-                regroup_scalar(i, t)
+            transpose_slabs(i, (0, 1))
+            regroup_scalar(i, 0)
             if i == 0:
                 sum_columns(0, (0, 1))
             elif live(i + 1):
@@ -240,7 +239,7 @@ def tile_hebbianlinear_pa_t_kernel(tc, x, wa, wb, wc, wd, weight_words, weight_s
                 transpose_wa()
             if live(i - 2):
                 matmul_1(i - 2)
-                sum_y(i - 2)
+                sum_y(i - 2, (0,))
                 round_y(i - 2)
             else:
                 keep_warm(1)
@@ -248,9 +247,8 @@ def tile_hebbianlinear_pa_t_kernel(tc, x, wa, wb, wc, wd, weight_words, weight_s
                 quantise_b(i - 1)
             if live(i - 2):
                 quantise_y(i - 2)
-            for t in (2, 3):
-                transpose_slabs(i, (t,))
-                regroup_scalar(i, t)
+            transpose_slabs(i, (2, 3))
+            regroup_scalar(i, 1)
             if i == 0:
                 sum_columns(0, (2, 3))
                 sum_columns(1, (0, 1, 2, 3))
@@ -258,6 +256,8 @@ def tile_hebbianlinear_pa_t_kernel(tc, x, wa, wb, wc, wd, weight_words, weight_s
                 sum_columns(i + 1, (2, 3))
             else:
                 start_rest()
+            if live(i - 2):
+                sum_y(i - 2, (1,))
             if live(i - 3):
                 matmul_2(i - 3)
             else:

@@ -231,10 +231,9 @@ def tile_hebbianlinear_pa_t_kernel(tc, x, wa, wb, wc, wd, weight_words, weight_s
             regroup_vector(i)
             transpose_slabs(i, (0, 1))
             regroup_scalar(i, 0)
-            if i == 0:
-                sum_columns(0, (0, 1))
-            elif live(i + 1):
-                sum_columns(i + 1, (0, 1))
+            summed = 0 if i == 0 else i + 1
+            if live(summed):
+                sum_columns(summed, (0,))
             else:
                 transpose_wa()
             if live(i - 2):
@@ -243,17 +242,16 @@ def tile_hebbianlinear_pa_t_kernel(tc, x, wa, wb, wc, wd, weight_words, weight_s
                 round_y(i - 2)
             else:
                 keep_warm(1)
+            if live(summed):
+                sum_columns(summed, (1,))
             if live(i - 1):
                 quantise_b(i - 1)
             if live(i - 2):
                 quantise_y(i - 2)
             transpose_slabs(i, (2, 3))
             regroup_scalar(i, 1)
-            if i == 0:
-                sum_columns(0, (2, 3))
-                sum_columns(1, (0, 1, 2, 3))
-            elif live(i + 1):
-                sum_columns(i + 1, (2, 3))
+            if live(summed):
+                sum_columns(summed, (2,))
             else:
                 start_rest()
             if live(i - 2):
@@ -262,6 +260,10 @@ def tile_hebbianlinear_pa_t_kernel(tc, x, wa, wb, wc, wd, weight_words, weight_s
                 matmul_2(i - 3)
             else:
                 keep_warm(1)
+            if live(summed):
+                sum_columns(summed, (3,))
+            if i == 0:
+                sum_columns(1, (0, 1, 2, 3))
 
         halves = [slice(h * N_TILE, (h + 1) * N_TILE) for h in range(N_HALVES)]
         x_mean = const.tile([P, IN_BLOCKS], F32)

@@ -36,6 +36,16 @@ def live(c):
     return 0 <= c < N_CHUNKS
 
 
+def a_parts(c):
+    return 2 if c == N_CHUNKS - 1 else 1
+
+
+def a_column(c, t, g):
+    rows = PACK // a_parts(c)
+    part, row = divmod(t, rows)
+    return ((part * IN_PASSES + g) * rows + row) * P
+
+
 def vector_cols(c):
     if c == 0:
         return FIRST_VECTOR_COLS
@@ -122,29 +132,40 @@ def tile_hebbianlinear_pa_t_kernel(tc, x, wa, wb, wc, wd, weight_words, weight_s
 
         def transpose_slabs(c, slabs):
             if c not in a_group:
-                a_group[c] = stage.tile([P, IN_PASSES, PACK, P, PACK], BF16, name="a_group", align_bytes=64)
+                parts = a_parts(c)
+                a_group[c] = stage.tile(
+                    [P, parts, IN_PASSES, PACK // parts, P, PACK], BF16, name="a_group", align_bytes=64
+                )
             for t in slabs:
                 words = x_tiles[c][:, t, :].bitcast(F32)
                 xt = psum_xt.tile([P, IN_PASSES, 2, P], F32, tag="xt")
                 for g in range(IN_PASSES):
                     for u in range(2):
                         nc.tensor.transpose(xt[:, g, u, :], words[:, 256 * g + u : 256 * (g + 1) : 2], ident[:])
-                nc.scalar.copy(out=a_group[c][:, :, t].bitcast(F32), in_=xt[:].rearrange("p g u b -> p g b u"))
+                part, row = divmod(t, PACK // a_parts(c))
+                nc.scalar.copy(
+                    out=a_group[c][:, part, :, row].bitcast(F32), in_=xt[:].rearrange("p g u b -> p g b u")
+                )
 
-        def quantise_a(c):
-            a_codes[c] = quant.tile([P, IN_PASSES * CHUNK], U32, name="a_codes", align_bytes=64)
-            a_scales[c] = quant.tile([P, IN_PASSES * CHUNK], U8, name="a_scales", align_bytes=64)
+        def quantise_a(c, part):
+            if c not in a_codes:
+                a_codes[c] = quant.tile([P, IN_PASSES * CHUNK], U32, name="a_codes", align_bytes=64)
+                a_scales[c] = quant.tile([P, IN_PASSES * CHUNK], U8, name="a_scales", align_bytes=64)
+            width = IN_PASSES * CHUNK // a_parts(c)
+            cols = slice(part * width, (part + 1) * width)
             nc.vector.quantize_mx(
-                out=a_codes[c][:].bitcast(FP8X4),
-                scales=a_scales[c][:],
-                in_=a_group[c][:].rearrange("p g t b k -> p (g t b k)"),
+                out=a_codes[c][:, cols].bitcast(FP8X4),
+                scales=a_scales[c][:, cols],
+                in_=a_group[c][:, part].rearrange("p g t b k -> p (g t b k)"),
             )
 
-        def matmul_1(c):
-            y_banks[c] = psum_y.tile([P, PACK, OUT], F32, name="y_bank", tag="y")
-            for t in range(PACK):
+        def matmul_1(c, slabs):
+            if c not in y_banks:
+                y_banks[c] = psum_y.tile([P, PACK, OUT], F32, name="y_bank", tag="y")
+            for t in slabs:
                 for g in range(IN_PASSES):
-                    cols = slice((g * PACK + t) * P, (g * PACK + t + 1) * P)
+                    first = a_column(c, t, g)
+                    cols = slice(first, first + P)
                     nc.tensor.matmul_mx(
                         out=y_banks[c][:, t, :],
                         lhsT=a_codes[c][:, cols].bitcast(FP8X4),
@@ -155,18 +176,22 @@ def tile_hebbianlinear_pa_t_kernel(tc, x, wa, wb, wc, wd, weight_words, weight_s
                         stop=(g == IN_PASSES - 1),
                     )
 
-        def sum_y(c, passes=(0, 1)):
-            for g in passes:
-                cols = slice(g * CHUNK, (g + 1) * CHUNK)
-                nc.tensor.matmul_mx(
-                    out=y_sum[:],
-                    lhsT=w_words[:, g, :].bitcast(FP4X4),
-                    lhsT_scale=w_scales[:, g, :],
-                    rhs=a_codes[c][:, cols].bitcast(FP8X4),
-                    rhs_scale=a_scales[c][:, cols],
-                    start=(c == 0 and g == 0),
-                    stop=(c == N_CHUNKS - 1 and g == IN_PASSES - 1),
-                )
+        def sum_y(c):
+            pieces = 1 if a_parts(c) == 1 else PACK
+            width = CHUNK // pieces
+            for piece in range(pieces):
+                for g in range(IN_PASSES):
+                    first = a_column(c, piece, g)
+                    cols = slice(first, first + width)
+                    nc.tensor.matmul_mx(
+                        out=y_sum[:, piece * width : (piece + 1) * width],
+                        lhsT=w_words[:, g, :].bitcast(FP4X4),
+                        lhsT_scale=w_scales[:, g, :],
+                        rhs=a_codes[c][:, cols].bitcast(FP8X4),
+                        rhs_scale=a_scales[c][:, cols],
+                        start=(c == 0 and g == 0),
+                        stop=(c == N_CHUNKS - 1 and g == IN_PASSES - 1 and piece == pieces - 1),
+                    )
 
         def round_y(c):
             y_group[c] = stage.tile([P, OUT, PACK], BF16, name="y_group", align_bytes=64)
@@ -199,18 +224,17 @@ def tile_hebbianlinear_pa_t_kernel(tc, x, wa, wb, wc, wd, weight_words, weight_s
                 in_=b_group[c][:].rearrange("p n t -> p (n t)"),
             )
 
-        def matmul_2(c):
-            for h in range(N_HALVES):
-                cols = slice(h * N_TILE, (h + 1) * N_TILE)
-                nc.tensor.matmul_mx(
-                    out=corr[h][:],
-                    lhsT=y_codes[c][:].bitcast(FP8X4),
-                    lhsT_scale=y_scales[c][:],
-                    rhs=b_codes[c][:, cols].bitcast(FP8X4),
-                    rhs_scale=b_scales[c][:, cols],
-                    start=(c == 0),
-                    stop=(c == N_CHUNKS - 1),
-                )
+        def matmul_2(c, h):
+            cols = slice(h * N_TILE, (h + 1) * N_TILE)
+            nc.tensor.matmul_mx(
+                out=corr[h][:],
+                lhsT=y_codes[c][:].bitcast(FP8X4),
+                lhsT_scale=y_scales[c][:],
+                rhs=b_codes[c][:, cols].bitcast(FP8X4),
+                rhs_scale=b_scales[c][:, cols],
+                start=(c == 0),
+                stop=(c == N_CHUNKS - 1),
+            )
 
         def regroup_vector(c):
             regroup_b(nc.vector.tensor_copy, c, 0, vector_cols(c))
@@ -225,7 +249,7 @@ def tile_hebbianlinear_pa_t_kernel(tc, x, wa, wb, wc, wd, weight_words, weight_s
             if live(i + LOAD_AHEAD):
                 load_x(i + LOAD_AHEAD, 1)
             if live(i - 1):
-                quantise_a(i - 1)
+                quantise_a(i - 1, 0)
             if i == LAST:
                 nc.vector.tensor_scalar_mul(out=x_mean[:], in0=x_sum[:, 0:IN_BLOCKS], scalar1=1.0 / BATCH)
             regroup_vector(i)
@@ -234,16 +258,17 @@ def tile_hebbianlinear_pa_t_kernel(tc, x, wa, wb, wc, wd, weight_words, weight_s
             summed = 0 if i == 0 else i + 1
             if live(summed):
                 sum_columns(summed, (0,))
-            else:
-                transpose_wa()
             if live(i - 2):
-                matmul_1(i - 2)
-                sum_y(i - 2, (0,))
+                sum_y(i - 2)
                 round_y(i - 2)
             else:
                 keep_warm(1)
+            if live(i - 3):
+                matmul_2(i - 3, 0)
             if live(summed):
                 sum_columns(summed, (1,))
+            else:
+                transpose_wa()
             if live(i - 1):
                 quantise_b(i - 1)
             if live(i - 2):
@@ -252,14 +277,12 @@ def tile_hebbianlinear_pa_t_kernel(tc, x, wa, wb, wc, wd, weight_words, weight_s
             regroup_scalar(i, 1)
             if live(summed):
                 sum_columns(summed, (2,))
-            else:
-                start_rest()
-            if live(i - 2):
-                sum_y(i - 2, (1,))
-            if live(i - 3):
-                matmul_2(i - 3)
+            if live(i - 1):
+                matmul_1(i - 1, range(PACK))
             else:
                 keep_warm(1)
+            if live(i - 3):
+                matmul_2(i - 3, 1)
             if live(summed):
                 sum_columns(summed, (3,))
             if i == 0:
@@ -315,35 +338,41 @@ def tile_hebbianlinear_pa_t_kernel(tc, x, wa, wb, wc, wd, weight_words, weight_s
         y_mean = const.tile([P, 1], F32)
         y_scaled = const.tile([P, N_TILE], F32)
 
-        quantise_a(LAST)
-        matmul_1(LAST - 1)
-        sum_y(LAST - 1)
+        quantise_a(LAST, 0)
         round_y(LAST - 1)
-        scale_wa(range(IN_BLOCKS))
-        matmul_2(LAST - 2)
+        quantise_a(LAST, 1)
+        start_rest()
+        matmul_2(LAST - 2, 0)
+        matmul_2(LAST - 2, 1)
+        matmul_1(LAST, range(PACK))
+        scale_wa(range(IN_BLOCKS // 2))
         quantise_y(LAST - 1)
         quantise_b(LAST)
-        matmul_1(LAST)
         round_y(LAST)
+        sum_y(LAST - 1)
         sum_y(LAST)
-        finish_rest()
         nc.scalar.activation(
             out=y_scaled[:], in_=y_sum[:], func=mybir.ActivationFunctionType.Copy, scale=1.0 / BATCH,
             accum_out=y_mean[:],
         )
-        matmul_2(LAST - 1)
+        scale_wa(range(IN_BLOCKS // 2, IN_BLOCKS))
+        matmul_2(LAST - 1, 0)
+        matmul_2(LAST - 1, 1)
         quantise_y(LAST)
-        matmul_2(LAST)
-        for h, cols in enumerate(halves):
-            nc.vector.scalar_tensor_tensor(
-                out=rest[:, cols], in0=wb_sb[:, cols], scalar=y_mean[:, 0:1], in1=rest_ps[h][:],
-                op0=ALU.mult, op1=ALU.add,
-            )
+        matmul_2(LAST, 0)
+        matmul_2(LAST, 1)
+        finish_rest()
 
         for cols, bank in zip(halves, corr):
             nc.vector.scalar_tensor_tensor(
                 out=result[:, cols], in0=bank[:], scalar=1.0 / BATCH, in1=wc_sb[:, cols],
                 op0=ALU.mult, op1=ALU.mult,
             )
+        for h, cols in enumerate(halves):
+            nc.vector.scalar_tensor_tensor(
+                out=rest[:, cols], in0=wb_sb[:, cols], scalar=y_mean[:, 0:1], in1=rest_ps[h][:],
+                op0=ALU.mult, op1=ALU.add,
+            )
+        for cols in halves:
             nc.vector.tensor_tensor(out=result[:, cols], in0=result[:, cols], in1=rest[:, cols], op=ALU.add)
             nc.sync.dma_start(out=out[:, cols], in_=result[:, cols])

@@ -97,8 +97,7 @@ def tile_hebbianlinear_pa_t_kernel(tc, x, wa, wb, wc, wd, weight_words, weight_s
             x_tiles[c] = x_sb
 
         load_x(0, PACK)
-        for c in range(1, 3):
-            load_x(c, 1)
+        load_x(1, 1)
         nc.sync.dma_start(
             out=w_words[:].bitcast(I32), in_=weight_words.bitcast(I32).rearrange("g p w -> p g w")
         )
@@ -108,7 +107,7 @@ def tile_hebbianlinear_pa_t_kernel(tc, x, wa, wb, wc, wd, weight_words, weight_s
                 in_=weight_scales.bitcast(I32)[:, 4 * quadrant : 4 * quadrant + 4, :].rearrange("g r w -> r g w"),
             )
 
-        for c in range(3, LOAD_AHEAD):
+        for c in range(2, LOAD_AHEAD):
             load_x(c, 1)
 
         corr = [psum_acc.tile([P, N_TILE], F32, name="corr%d" % h) for h in range(N_HALVES)]
@@ -248,6 +247,8 @@ def tile_hebbianlinear_pa_t_kernel(tc, x, wa, wb, wc, wd, weight_words, weight_s
         def step(i):
             if live(i + LOAD_AHEAD):
                 load_x(i + LOAD_AHEAD, 1)
+            if live(i - 2):
+                round_y(i - 2)
             if live(i - 1):
                 quantise_a(i - 1, 0)
             if i == LAST:
@@ -260,7 +261,6 @@ def tile_hebbianlinear_pa_t_kernel(tc, x, wa, wb, wc, wd, weight_words, weight_s
                 sum_columns(summed, (0,))
             if live(i - 2):
                 sum_y(i - 2)
-                round_y(i - 2)
             else:
                 keep_warm(1)
             if live(i - 3):
@@ -269,12 +269,15 @@ def tile_hebbianlinear_pa_t_kernel(tc, x, wa, wb, wc, wd, weight_words, weight_s
                 sum_columns(summed, (1,))
             else:
                 transpose_wa()
-            if live(i - 1):
-                quantise_b(i - 1)
             if live(i - 2):
                 quantise_y(i - 2)
+            if i == LAST:
+                quantise_a(LAST, 0)
+            if live(i - 1):
+                quantise_b(i - 1)
             transpose_slabs(i, (2, 3))
-            regroup_scalar(i, 1)
+            if i < LAST:
+                regroup_scalar(i, 1)
             if live(summed):
                 sum_columns(summed, (2,))
             if live(i - 1):
@@ -338,29 +341,29 @@ def tile_hebbianlinear_pa_t_kernel(tc, x, wa, wb, wc, wd, weight_words, weight_s
         y_mean = const.tile([P, 1], F32)
         y_scaled = const.tile([P, N_TILE], F32)
 
-        quantise_a(LAST, 0)
-        round_y(LAST - 1)
         quantise_a(LAST, 1)
-        start_rest()
+        round_y(LAST - 1)
+        regroup_scalar(LAST, 1)
         matmul_2(LAST - 2, 0)
         matmul_2(LAST - 2, 1)
+        sum_y(LAST - 1)
         matmul_1(LAST, range(PACK))
         scale_wa(range(IN_BLOCKS // 2))
         quantise_y(LAST - 1)
         quantise_b(LAST)
         round_y(LAST)
-        sum_y(LAST - 1)
+        matmul_2(LAST - 1, 0)
+        matmul_2(LAST - 1, 1)
         sum_y(LAST)
         nc.scalar.activation(
             out=y_scaled[:], in_=y_sum[:], func=mybir.ActivationFunctionType.Copy, scale=1.0 / BATCH,
             accum_out=y_mean[:],
         )
         scale_wa(range(IN_BLOCKS // 2, IN_BLOCKS))
-        matmul_2(LAST - 1, 0)
-        matmul_2(LAST - 1, 1)
         quantise_y(LAST)
         matmul_2(LAST, 0)
         matmul_2(LAST, 1)
+        start_rest()
         finish_rest()
 
         for cols, bank in zip(halves, corr):

@@ -24,7 +24,7 @@ IN_BLOCKS = IN // P
 N_TILE = 512
 N_HALVES = IN // N_TILE
 
-VECTOR_COLS = 688
+VECTOR_COLS = 720
 FIRST_VECTOR_COLS = 960
 SUM_COLS = 16
 LOAD_AHEAD = 6
@@ -249,11 +249,11 @@ def tile_hebbianlinear_pa_t_kernel(tc, x, wa, wb, wc, wd, weight_words, weight_s
                 load_x(i + LOAD_AHEAD, 1)
             if live(i - 2):
                 round_y(i - 2)
-            if live(i - 1):
-                quantise_a(i - 1, 0)
             if i == LAST:
                 nc.vector.tensor_scalar_mul(out=x_mean[:], in0=x_sum[:, 0:IN_BLOCKS], scalar1=1.0 / BATCH)
             regroup_vector(i)
+            if live(i - 1):
+                quantise_a(i - 1, 0)
             transpose_slabs(i, (0, 1))
             regroup_scalar(i, 0)
             summed = 0 if i == 0 else i + 1

@@ -25,7 +25,7 @@ N_TILE = 512
 N_HALVES = IN // N_TILE
 
 VECTOR_COLS = 720
-FIRST_VECTOR_COLS = 960
+FIRST_VECTOR_COLS = 832
 SUM_COLS = 16
 LOAD_AHEAD = 6
 
@@ -250,13 +250,17 @@ def tile_hebbianlinear_pa_t_kernel(tc, x, wa, wb, wc, wd, weight_words, weight_s
             if live(i - 2):
                 round_y(i - 2)
             if i == LAST:
-                nc.vector.tensor_scalar_mul(out=x_mean[:], in0=x_sum[:, 0:IN_BLOCKS], scalar1=1.0 / BATCH)
+                nc.scalar.activation(
+                    out=x_mean[:], in_=x_sum[:, 0:IN_BLOCKS], func=mybir.ActivationFunctionType.Copy, scale=1.0 / BATCH
+                )
+            if i == 1:
+                quantise_a(0, 0)
             regroup_vector(i)
-            if live(i - 1):
+            if i > 1:
                 quantise_a(i - 1, 0)
             transpose_slabs(i, (0, 1))
             regroup_scalar(i, 0)
-            summed = 0 if i == 0 else i + 1
+            summed = i if i < 2 else i + 1
             if live(summed):
                 sum_columns(summed, (0,))
             if live(i - 2):
@@ -288,8 +292,8 @@ def tile_hebbianlinear_pa_t_kernel(tc, x, wa, wb, wc, wd, weight_words, weight_s
                 matmul_2(i - 3, 1)
             if live(summed):
                 sum_columns(summed, (3,))
-            if i == 0:
-                sum_columns(1, (0, 1, 2, 3))
+            if i == 1:
+                sum_columns(2, range(PACK))
 
         halves = [slice(h * N_TILE, (h + 1) * N_TILE) for h in range(N_HALVES)]
         x_mean = const.tile([P, IN_BLOCKS], F32)

@@ -24,7 +24,7 @@ IN_BLOCKS = IN // P
 N_TILE = 512
 N_HALVES = IN // N_TILE
 
-VECTOR_COLS = 720
+VECTOR_COLS = 696
 FIRST_VECTOR_COLS = 832
 SUM_COLS = 16
 LOAD_AHEAD = 6

@@ -72,7 +72,7 @@ def tile_hebbianlinear_pa_t_kernel(tc, x, wa, wb, wc, wd, weight_words, weight_s
             for repeat in range(count):
                 nc.tensor.matmul(out=warm[:], lhsT=zeros[:, 0:P], rhs=zeros[:], start=True, stop=True)
 
-        keep_warm(2)
+        keep_warm(4)
 
         ident = const.tile([P, P], F32)
         make_identity(nc, ident[:])

from contextlib import ExitStack

import concourse.mybir as mybir
from concourse.masks import make_identity

F32 = mybir.dt.float32
BF16 = mybir.dt.bfloat16
I32 = mybir.dt.int32
U32 = mybir.dt.uint32
U8 = mybir.dt.uint8
FP8X4 = mybir.dt.float8_e4m3fn_x4
FP4X4 = mybir.dt.float4_e2m1fn_x4
ALU = mybir.AluOpType

P = 128
PACK = 4
K_PASS = P * PACK

BATCH, IN, OUT = 8192, 1024, 128
CHUNK = K_PASS
N_CHUNKS = BATCH // CHUNK
IN_PASSES = IN // K_PASS
IN_BLOCKS = IN // P
N_TILE = 512
N_HALVES = IN // N_TILE

VECTOR_COLS = 696
FIRST_VECTOR_COLS = 832
SUM_COLS = 16
LOAD_AHEAD = 6

FLOPS = 2 * 2 * BATCH * IN * OUT


def live(c):
    return 0 <= c < N_CHUNKS


def a_parts(c):
    return 2 if c == N_CHUNKS - 1 else 1


def a_column(c, t, g):
    rows = PACK // a_parts(c)
    part, row = divmod(t, rows)
    return ((part * IN_PASSES + g) * rows + row) * P


def vector_cols(c):
    if c == 0:
        return FIRST_VECTOR_COLS
    return VECTOR_COLS


def tile_hebbianlinear_pa_t_kernel(tc, x, wa, wb, wc, wd, weight_words, weight_scales, out):
    nc = tc.nc
    with ExitStack() as ctx:
        const = ctx.enter_context(tc.tile_pool(name="const", bufs=1))
        x_pool = ctx.enter_context(tc.tile_pool(name="x", bufs=LOAD_AHEAD + 1))
        stage = ctx.enter_context(tc.tile_pool(name="stage", bufs=4))
        quant = ctx.enter_context(tc.tile_pool(name="quant", bufs=5))
        psum_xt = ctx.enter_context(tc.psum_pool(name="psum_xt", bufs=3))
        psum_y = ctx.enter_context(tc.psum_pool(name="psum_y", bufs=1))
        psum_acc = ctx.enter_context(tc.psum_pool(name="psum_acc", bufs=1))
        ctx.enter_context(tc.manual_schedule())

        zeros = const.tile([P, N_TILE], BF16)
        nc.vector.memset(zeros[:], 0.0)

        def keep_warm(count):
            warm = psum_y.tile([P, N_TILE], F32, name="warm", tag="y")
            for repeat in range(count):
                nc.tensor.matmul(out=warm[:], lhsT=zeros[:, 0:P], rhs=zeros[:], start=True, stop=True)

        keep_warm(4)

        ident = const.tile([P, P], F32)
        make_identity(nc, ident[:])
        ident_bf = const.tile([P, P], BF16)
        make_identity(nc, ident_bf[:])
        pick = const.tile([P, IN_BLOCKS, SUM_COLS], BF16)
        nc.vector.memset(pick[:], 0.0)
        nc.vector.memset(pick[:].rearrange("p a b -> p (a b)")[:, 0 : IN_BLOCKS * SUM_COLS : SUM_COLS + 1], 1.0)

        w_words = const.tile([P, IN_PASSES, 2 * OUT], U8, align_bytes=64)
        w_scales = const.tile([P, IN_PASSES, OUT], U8, align_bytes=64)
        nc.vector.memset(w_scales[:].rearrange("p g n -> p (g n)").bitcast(I32), 0)

        x_tiles = {}

        def load_x(c, pieces):
            x_sb = x_pool.tile([P, PACK, IN], BF16)
            rows = x[c * CHUNK : (c + 1) * CHUNK, :].rearrange("(p t) n -> p t n", t=PACK)
            step_t = PACK // pieces
            for t in range(0, PACK, step_t):
                nc.sync.dma_start(out=x_sb[:, t : t + step_t, :], in_=rows[:, t : t + step_t, :])
            x_tiles[c] = x_sb

        load_x(0, PACK)
        load_x(1, 1)
        nc.sync.dma_start(
            out=w_words[:].bitcast(I32), in_=weight_words.bitcast(I32).rearrange("g p w -> p g w")
        )
        for quadrant in range(4):
            nc.sync.dma_start(
                out=w_scales[32 * quadrant : 32 * quadrant + 4].bitcast(I32),
                in_=weight_scales.bitcast(I32)[:, 4 * quadrant : 4 * quadrant + 4, :].rearrange("g r w -> r g w"),
            )

        for c in range(2, LOAD_AHEAD):
            load_x(c, 1)

        corr = [psum_acc.tile([P, N_TILE], F32, name="corr%d" % h) for h in range(N_HALVES)]
        x_sum = psum_acc.tile([P, N_TILE], F32, tag="x_sum")
        y_sum = psum_acc.tile([P, N_TILE], F32, tag="y_sum")

        a_group, a_codes, a_scales = {}, {}, {}
        b_group, b_codes, b_scales = {}, {}, {}
        y_banks, y_group, y_codes, y_scales = {}, {}, {}, {}

        def sum_columns(c, slabs):
            for t in slabs:
                for j in range(IN_BLOCKS):
                    nc.tensor.matmul(
                        out=x_sum[:, 0:SUM_COLS],
                        lhsT=x_tiles[c][:, t, j * P : (j + 1) * P],
                        rhs=pick[:, j, :],
                        start=(c == 0 and t == 0 and j == 0),
                        stop=(c == N_CHUNKS - 1 and t == PACK - 1 and j == IN_BLOCKS - 1),
                    )

        def transpose_slabs(c, slabs):
            if c not in a_group:
                parts = a_parts(c)
                a_group[c] = stage.tile(
                    [P, parts, IN_PASSES, PACK // parts, P, PACK], BF16, name="a_group", align_bytes=64
                )
            for t in slabs:
                words = x_tiles[c][:, t, :].bitcast(F32)
                xt = psum_xt.tile([P, IN_PASSES, 2, P], F32, tag="xt")
                for g in range(IN_PASSES):
                    for u in range(2):
                        nc.tensor.transpose(xt[:, g, u, :], words[:, 256 * g + u : 256 * (g + 1) : 2], ident[:])
                part, row = divmod(t, PACK // a_parts(c))
                nc.scalar.copy(
                    out=a_group[c][:, part, :, row].bitcast(F32), in_=xt[:].rearrange("p g u b -> p g b u")
                )

        def quantise_a(c, part):
            if c not in a_codes:
                a_codes[c] = quant.tile([P, IN_PASSES * CHUNK], U32, name="a_codes", align_bytes=64)
                a_scales[c] = quant.tile([P, IN_PASSES * CHUNK], U8, name="a_scales", align_bytes=64)
            width = IN_PASSES * CHUNK // a_parts(c)
            cols = slice(part * width, (part + 1) * width)
            nc.vector.quantize_mx(
                out=a_codes[c][:, cols].bitcast(FP8X4),
                scales=a_scales[c][:, cols],
                in_=a_group[c][:, part].rearrange("p g t b k -> p (g t b k)"),
            )

        def matmul_1(c, slabs):
            if c not in y_banks:
                y_banks[c] = psum_y.tile([P, PACK, OUT], F32, name="y_bank", tag="y")
            for t in slabs:
                for g in range(IN_PASSES):
                    first = a_column(c, t, g)
                    cols = slice(first, first + P)
                    nc.tensor.matmul_mx(
                        out=y_banks[c][:, t, :],
                        lhsT=a_codes[c][:, cols].bitcast(FP8X4),
                        lhsT_scale=a_scales[c][:, cols],
                        rhs=w_words[:, g, :].bitcast(FP4X4),
                        rhs_scale=w_scales[:, g, :],
                        start=(g == 0),
                        stop=(g == IN_PASSES - 1),
                    )

        def sum_y(c):
            pieces = 1 if a_parts(c) == 1 else PACK
            width = CHUNK // pieces
            for piece in range(pieces):
                for g in range(IN_PASSES):
                    first = a_column(c, piece, g)
                    cols = slice(first, first + width)
                    nc.tensor.matmul_mx(
                        out=y_sum[:, piece * width : (piece + 1) * width],
                        lhsT=w_words[:, g, :].bitcast(FP4X4),
                        lhsT_scale=w_scales[:, g, :],
                        rhs=a_codes[c][:, cols].bitcast(FP8X4),
                        rhs_scale=a_scales[c][:, cols],
                        start=(c == 0 and g == 0),
                        stop=(c == N_CHUNKS - 1 and g == IN_PASSES - 1 and piece == pieces - 1),
                    )

        def round_y(c):
            y_group[c] = stage.tile([P, OUT, PACK], BF16, name="y_group", align_bytes=64)
            nc.scalar.copy(out=y_group[c][:], in_=y_banks[c][:].rearrange("p t o -> p o t"))

        def quantise_y(c):
            y_codes[c] = quant.tile([P, OUT], U32, name="y_codes", align_bytes=64)
            y_scales[c] = quant.tile([P, OUT], U8, name="y_scales", align_bytes=64)
            nc.vector.quantize_mx(
                out=y_codes[c][:].bitcast(FP8X4),
                scales=y_scales[c][:],
                in_=y_group[c][:].rearrange("p o t -> p (o t)"),
            )

        def regroup_b(engine_copy, c, first, count):
            if c not in b_group:
                b_group[c] = stage.tile([P, IN, PACK], BF16, name="b_group", align_bytes=64)
            cols = slice(first, first + count)
            engine_copy(
                out=b_group[c][:, cols, :].rearrange("p (n i) t -> p n t i", i=4),
                in_=x_tiles[c][:, :, cols].rearrange("p t (n i) -> p n t i", i=4),
            )

        def quantise_b(c):
            b_codes[c] = quant.tile([P, IN], U32, name="b_codes", align_bytes=64)
            b_scales[c] = quant.tile([P, IN], U8, name="b_scales", align_bytes=64)
            nc.vector.quantize_mx(
                out=b_codes[c][:].bitcast(FP8X4),
                scales=b_scales[c][:],
                in_=b_group[c][:].rearrange("p n t -> p (n t)"),
            )

        def matmul_2(c, h):
            cols = slice(h * N_TILE, (h + 1) * N_TILE)
            nc.tensor.matmul_mx(
                out=corr[h][:],
                lhsT=y_codes[c][:].bitcast(FP8X4),
                lhsT_scale=y_scales[c][:],
                rhs=b_codes[c][:, cols].bitcast(FP8X4),
                rhs_scale=b_scales[c][:, cols],
                start=(c == 0),
                stop=(c == N_CHUNKS - 1),
            )

        def regroup_vector(c):
            regroup_b(nc.vector.tensor_copy, c, 0, vector_cols(c))

        def regroup_scalar(c, piece):
            count = (IN - vector_cols(c)) // 2
            regroup_b(nc.scalar.copy, c, vector_cols(c) + piece * count, count)

        LAST = N_CHUNKS - 1

        def step(i):
            if live(i + LOAD_AHEAD):
                load_x(i + LOAD_AHEAD, 1)
            if live(i - 2):
                round_y(i - 2)
            if i == LAST:
                nc.scalar.activation(
                    out=x_mean[:], in_=x_sum[:, 0:IN_BLOCKS], func=mybir.ActivationFunctionType.Copy, scale=1.0 / BATCH
                )
            if i == 1:
                quantise_a(0, 0)
            regroup_vector(i)
            if i > 1:
                quantise_a(i - 1, 0)
            transpose_slabs(i, (0, 1))
            regroup_scalar(i, 0)
            summed = i if i < 2 else i + 1
            if live(summed):
                sum_columns(summed, (0,))
            if live(i - 2):
                sum_y(i - 2)
            else:
                keep_warm(1)
            if live(i - 3):
                matmul_2(i - 3, 0)
            if live(summed):
                sum_columns(summed, (1,))
            else:
                transpose_wa()
            if live(i - 2):
                quantise_y(i - 2)
            if i == LAST:
                quantise_a(LAST, 0)
            if live(i - 1):
                quantise_b(i - 1)
            transpose_slabs(i, (2, 3))
            if i < LAST:
                regroup_scalar(i, 1)
            if live(summed):
                sum_columns(summed, (2,))
            if live(i - 1):
                matmul_1(i - 1, range(PACK))
            else:
                keep_warm(1)
            if live(i - 3):
                matmul_2(i - 3, 1)
            if live(summed):
                sum_columns(summed, (3,))
            if i == 1:
                sum_columns(2, range(PACK))

        halves = [slice(h * N_TILE, (h + 1) * N_TILE) for h in range(N_HALVES)]
        x_mean = const.tile([P, IN_BLOCKS], F32)
        wa_sb = const.tile([P, IN], BF16)
        wb_sb = const.tile([P, IN], BF16)
        wc_sb = const.tile([P, IN], BF16)
        wd_sb = const.tile([P, IN], BF16)
        wa_t, rest_ps = {}, {}
        xa_t = const.tile([P, IN_BLOCKS, P], F32)

        def transpose_wa():
            wa_t[0] = psum_acc.tile([P, IN_BLOCKS, P], BF16, name="wa_t", tag="x_sum")
            for j in range(IN_BLOCKS):
                nc.tensor.transpose(wa_t[0][:, j, :], wa_sb[:, j * P : (j + 1) * P], ident_bf[:])

        def start_rest():
            for h, cols in enumerate(halves):
                rest_ps[h] = psum_xt.tile([P, N_TILE], F32, name="rest_ps%d" % h, tag="xt")
                nc.tensor.matmul(out=rest_ps[h][:], lhsT=ident_bf[:], rhs=wd_sb[:, cols], start=True, stop=False)

        def scale_wa(blocks):
            for j in blocks:
                nc.scalar.activation(
                    out=xa_t[:, j, :], in_=wa_t[0][:, j, :], func=mybir.ActivationFunctionType.Copy,
                    scale=x_mean[:, j : j + 1],
                )

        def finish_rest():
            for j in range(IN_BLOCKS):
                h, q = divmod(j, N_TILE // P)
                nc.tensor.matmul(
                    out=rest_ps[h][:, q * P : (q + 1) * P], lhsT=xa_t[:, j, :], rhs=ident[:], is_transpose=True,
                    start=False, stop=(q == N_TILE // P - 1),
                )

        for i in range(0, N_CHUNKS - LOAD_AHEAD):
            step(i)

        nc.sync.dma_start(out=wa_sb[:], in_=wa)
        nc.sync.dma_start(out=wd_sb[:], in_=wd)
        nc.sync.dma_start(out=wb_sb[:], in_=wb)
        nc.sync.dma_start(out=wc_sb[:], in_=wc)

        for i in range(N_CHUNKS - LOAD_AHEAD, N_CHUNKS):
            step(i)

        rest = const.tile([P, IN], F32)
        result = const.tile([P, IN], F32)
        y_mean = const.tile([P, 1], F32)
        y_scaled = const.tile([P, N_TILE], F32)

        quantise_a(LAST, 1)
        round_y(LAST - 1)
        regroup_scalar(LAST, 1)
        matmul_2(LAST - 2, 0)
        matmul_2(LAST - 2, 1)
        sum_y(LAST - 1)
        matmul_1(LAST, range(PACK))
        scale_wa(range(IN_BLOCKS // 2))
        quantise_y(LAST - 1)
        quantise_b(LAST)
        round_y(LAST)
        matmul_2(LAST - 1, 0)
        matmul_2(LAST - 1, 1)
        sum_y(LAST)
        nc.scalar.activation(
            out=y_scaled[:], in_=y_sum[:], func=mybir.ActivationFunctionType.Copy, scale=1.0 / BATCH,
            accum_out=y_mean[:],
        )
        scale_wa(range(IN_BLOCKS // 2, IN_BLOCKS))
        quantise_y(LAST)
        matmul_2(LAST, 0)
        matmul_2(LAST, 1)
        start_rest()
        finish_rest()

        for cols, bank in zip(halves, corr):
            nc.vector.scalar_tensor_tensor(
                out=result[:, cols], in0=bank[:], scalar=1.0 / BATCH, in1=wc_sb[:, cols],
                op0=ALU.mult, op1=ALU.mult,
            )
        for h, cols in enumerate(halves):
            nc.vector.scalar_tensor_tensor(
                out=rest[:, cols], in0=wb_sb[:, cols], scalar=y_mean[:, 0:1], in1=rest_ps[h][:],
                op0=ALU.mult, op1=ALU.add,
            )
        for cols in halves:
            nc.vector.tensor_tensor(out=result[:, cols], in0=result[:, cols], in1=rest[:, cols], op=ALU.add)
            nc.sync.dma_start(out=out[:, cols], in_=result[:, cols])
